import numpy as np
import ml_dtypes


def mxq(x, axis, fmt="e4m3"):
    dtype, down = {"e4m3": (ml_dtypes.float8_e4m3fn, 7), "e5m2": (ml_dtypes.float8_e5m2, 14)}[fmt]
    v = np.moveaxis(np.asarray(x, np.float32).astype(ml_dtypes.bfloat16).astype(np.float64), axis, -1)
    blocks = v.reshape(v.shape[:-1] + (-1, 32))
    amax = np.abs(blocks).max(-1, keepdims=True)
    byte = np.maximum(np.where(amax > 0, np.frexp(amax)[1] - 1 + 127, 0) - down, 1)
    scale = np.exp2(byte - 127.0)
    codes = (blocks / scale).astype(np.float32).astype(dtype).astype(np.float64)
    return np.moveaxis((codes * scale).reshape(v.shape), -1, axis)


WIDE = False


def mx_kscale(k):
    if not WIDE:
        return np.ones(k)
    levels = np.array([10, -10, 5, -5, 0])
    a = np.random.permutation(np.resize(levels, k // 512 * 4)).reshape(k // 512, 4)
    idx = np.arange(k)
    return np.exp2(a[idx // 512, idx % 128 // 32])


BF16 = ml_dtypes.bfloat16


def bf(x):
    return np.asarray(x, np.float32).astype(BF16)


def f64(x):
    return np.asarray(x).astype(np.float64)


E2M1 = np.array([0.0, 0.5, 1.0, 1.5, 2.0, 3.0, 4.0, 6.0, -0.0, -0.5, -1.0, -1.5, -2.0, -3.0, -4.0, -6.0])


def pack_weight(w, fmt):
    k, n = w.shape
    w = f64(bf(w)).reshape(k // 32, 32, n)
    amax = np.abs(w).max(1)
    if fmt == "e4m3":
        byte = np.frexp(amax)[1] - 1 + 127 - 7
    else:
        mant, ex = np.frexp(amax / 6.0)
        byte = np.where(mant > 0.5, ex, ex - 1) + 127
    byte = np.clip(np.where(amax > 0, byte, 1), 1, 254)
    scaled = (w * np.exp2(127.0 - byte)[:, None, :]).reshape(k, n).astype(np.float32)
    by_word = np.ascontiguousarray(scaled.reshape(k // 512, 128, 4, n).transpose(0, 1, 3, 2))
    if fmt == "e4m3":
        words = by_word.astype(ml_dtypes.float8_e4m3fn).view(np.uint8)
    else:
        c = by_word.astype(ml_dtypes.float4_e2m1fn).view(np.uint8) & 0xF
        words = c[..., 0::2] | (c[..., 1::2] << 4)
    return np.ascontiguousarray(words), np.ascontiguousarray(byte.astype(np.uint8).reshape(k // 512, 16, n))


def unpack_weight(words, scales, fmt):
    g, p, n, _ = words.shape
    if fmt == "e4m3":
        vals = np.ascontiguousarray(words).view(ml_dtypes.float8_e4m3fn).astype(np.float64)
    else:
        nib = np.empty((g, p, n, 4), np.uint8)
        nib[..., 0::2] = words & 0xF
        nib[..., 1::2] = words >> 4
        vals = E2M1[nib]
    vals = vals * np.repeat(np.exp2(scales.astype(np.float64) - 127.0), 8, axis=1)[..., None]
    return vals.transpose(0, 1, 3, 2).reshape(g * 512, n)

def pack4(w):
    words, scales = pack_weight(w, "e2m1")
    return words.reshape(words.shape[0], 128, -1), scales


def unpack4(words, scales):
    return unpack_weight(words.reshape(words.shape[0], 128, -1, 2), scales, "e2m1")


B, H = 4096, 512
K = 2 * H
BETA_SHIFT = 1.0
LN_EPS = 1e-5
BAG_EPS = 1e-6


def setup_inputs():
    s = mx_kscale(H)
    r_main = np.random.uniform(0.5, 1.1, (B, 1))
    r_branch = np.random.uniform(0.5, 1.1, (B, 1))
    w_mb = np.random.standard_normal((K, H)) / np.sqrt(K)
    w_mb[H:] = w_mb[H:] / s[:, None]
    main = bf(np.random.standard_normal((B, H)) * r_main)
    branch = bf(np.random.standard_normal((B, H)) * r_branch * s)
    o = bf(1.0 - np.random.random((B, 1)) * np.random.uniform(0.2, 0.8, (B, H)))
    is_bag = bf(np.random.random((B, 1)))
    W_mb_words, W_mb_scales = pack4(w_mb)
    b_mb = bf(np.random.standard_normal(H) * 0.3)
    W_b_words, W_b_scales = pack4(np.random.standard_normal((H, H)) * 2.0 / np.sqrt(H) / s[:, None])
    b_b = bf(np.random.standard_normal(H) * 0.3)
    ln_g = bf(1.0 + 0.1 * np.random.standard_normal(H))
    ln_b = bf(0.1 * np.random.standard_normal(H))
    return {"main": main,
            "branch": branch,
            "o": o,
            "is_bag": is_bag,
            "W_mb_words": W_mb_words,
            "W_mb_scales": W_mb_scales,
            "b_mb": b_mb,
            "W_b_words": W_b_words,
            "W_b_scales": W_b_scales,
            "b_b": b_b,
            "ln_g": ln_g,
            "ln_b": ln_b}


def reference(main, branch, o, is_bag, W_mb_words, W_mb_scales, b_mb, W_b_words, W_b_scales, b_b, ln_g, ln_b):
    main, is_bag = f64(main), f64(is_bag)
    mbq = mxq(np.concatenate([main, f64(branch)], axis=-1), 1, "e4m3")
    weight_b = np.maximum((mbq @ unpack4(W_mb_words, W_mb_scales)) + f64(b_mb), 0.0)
    h_m = weight_b * ((mbq[:, H:] @ unpack4(W_b_words, W_b_scales)) + f64(b_b))
    em_norm = np.sqrt((main ** 2).sum(-1))
    hm_norm = np.sqrt((h_m ** 2).sum(-1))
    hm_norm = np.where(hm_norm == 0, np.ones_like(hm_norm), hm_norm)
    alpha = np.minimum(em_norm / (hm_norm + BAG_EPS) * BETA_SHIFT, 1.0)[:, None]
    pre = alpha * h_m + main
    mu = pre.mean(-1, keepdims=True)
    var = ((pre - mu) ** 2).mean(-1, keepdims=True)
    emb = (pre - mu) / np.sqrt(var + LN_EPS) * f64(ln_g) + f64(ln_b)
    shift_c = emb * is_bag + main * (1.0 - is_bag)
    h = f64(o) * np.tanh(shift_c)
    return h, shift_c

@@ -1,0 +1,270 @@
+from contextlib import ExitStack
+
+import concourse.mybir as mybir
+from concourse.masks import make_identity
+
+F32 = mybir.dt.float32
+BF16 = mybir.dt.bfloat16
+I32 = mybir.dt.int32
+U8 = mybir.dt.uint8
+U32 = mybir.dt.uint32
+FP8X4 = mybir.dt.float8_e4m3fn_x4
+FP4X4 = mybir.dt.float4_e2m1fn_x4
+ALU = mybir.AluOpType
+ACT = mybir.ActivationFunctionType
+
+P = 128
+B, H = 4096, 512
+TILES = B // P
+GROUP = 4
+GROUPS = TILES // GROUP
+ROWS = GROUP * P
+CHUNKS = H // P
+PASSES = 3
+LN_EPS = 1e-5
+BAG_EPS = 1e-6
+BETA_SHIFT = 1.0
+LOAD_AHEAD = 2
+
+FLOPS = 2 * B * (2 * H + H) * H
+
+
+def tile_bag_lstm_pb_t_kernel(
+    tc, main, branch, o, is_bag, W_mb_words, W_mb_scales, b_mb, W_b_words, W_b_scales, b_b, ln_g, ln_b, out_0, out_1
+):
+    nc = tc.nc
+    main_v = main.rearrange("(p t) f -> p t f", t=TILES)
+    branch_v = branch.rearrange("(p t) f -> p t f", t=TILES)
+    o_v = o.rearrange("(p t) f -> p t f", t=TILES)
+    h_v = out_0.rearrange("(p t) f -> p t f", t=TILES)
+    shift_v = out_1.rearrange("(p t) f -> p t f", t=TILES)
+
+    with ExitStack() as ctx:
+        consts = ctx.enter_context(tc.tile_pool(name="consts", bufs=1))
+        inputs = ctx.enter_context(tc.tile_pool(name="inputs", bufs=3))
+        work = ctx.enter_context(tc.tile_pool(name="work", bufs=2))
+        small = ctx.enter_context(tc.tile_pool(name="small", bufs=3))
+        psum = ctx.enter_context(tc.psum_pool(name="psum", bufs=2))
+
+        main_of, branch_of, o_of = {}, {}, {}
+        hT_of, em_of, wm_of, pre_of, negmu_of, rstd_of = {}, {}, {}, {}, {}, {}
+
+        def load(g):
+            rows = slice(g * GROUP, (g + 1) * GROUP)
+            main_sb = inputs.tile([P, GROUP, H], BF16, tag="main", bufs=4)
+            nc.sync.dma_start(out=main_sb[:], in_=main_v[:, rows, :])
+            branch_sb = inputs.tile([P, GROUP, H], BF16, tag="branch", bufs=3)
+            nc.sync.dma_start(out=branch_sb[:], in_=branch_v[:, rows, :])
+            main_of[g], branch_of[g] = main_sb, branch_sb
+
+        def load_o(g):
+            o_sb = inputs.tile([P, GROUP, H], BF16, tag="o", bufs=3)
+            nc.sync.dma_start(out=o_sb[:], in_=o_v[:, g * GROUP : (g + 1) * GROUP, :])
+            o_of[g] = o_sb
+
+        bias_rows = consts.tile([P, P], BF16)
+        nc.vector.memset(bias_rows[:], 0.0)
+        nc.scalar.dma_start(out=bias_rows[0:CHUNKS, :], in_=b_mb.rearrange("(c p) -> c p", p=P))
+        nc.scalar.dma_start(out=bias_rows[CHUNKS : 2 * CHUNKS, :], in_=b_b.rearrange("(c p) -> c p", p=P))
+        bag_bf = consts.tile([P, TILES], BF16)
+        nc.scalar.dma_start(out=bag_bf[:], in_=is_bag.rearrange("(p t) o -> p (t o)", t=TILES))
+
+        load(0)
+
+        ident = consts.tile([P, P], F32)
+        make_identity(nc, ident[:])
+
+        w_words = consts.tile([P, PASSES, 2 * H], U8, align_bytes=64)
+        nc.sync.dma_start(out=w_words[:, 0:2, :].bitcast(I32), in_=W_mb_words.rearrange("g p b -> p g b").bitcast(I32))
+        nc.sync.dma_start(out=w_words[:, 2, :].bitcast(I32), in_=W_b_words[0].bitcast(I32))
+        w_scales = consts.tile([P, PASSES, H], U8, align_bytes=64)
+        nc.vector.memset(w_scales[:].bitcast(I32), 0)
+        for quad in range(4):
+            live = slice(32 * quad, 32 * quad + 4)
+            q_rows = slice(4 * quad, 4 * quad + 4)
+            nc.sync.dma_start(
+                out=w_scales[live, 0:2, :].bitcast(I32),
+                in_=W_mb_scales[:, q_rows, :].rearrange("g q n -> q g n").bitcast(I32),
+            )
+            nc.sync.dma_start(out=w_scales[live, 2, :].bitcast(I32), in_=W_b_scales[0, q_rows, :].bitcast(I32))
+
+        for g in range(1, LOAD_AHEAD):
+            load(g)
+
+        gain = consts.tile([P, H], BF16)
+        nc.scalar.dma_start(out=gain[:], in_=ln_g.partition_broadcast(P))
+        shift = consts.tile([P, H], BF16)
+        nc.scalar.dma_start(out=shift[:], in_=ln_b.partition_broadcast(P))
+
+        bag = consts.tile([P, TILES], F32)
+        nc.vector.tensor_copy(out=bag[:], in_=bag_bf[:])
+        one_minus_bag = consts.tile([P, TILES], F32)
+        nc.vector.tensor_scalar(out=one_minus_bag[:], in0=bag[:], scalar1=-1.0, scalar2=1.0, op0=ALU.mult, op1=ALU.add)
+
+        half = consts.tile([P, GROUP], F32)
+        nc.gpsimd.memset(half[:], 0.5)
+        minus_half = consts.tile([P, GROUP], F32)
+        nc.gpsimd.memset(minus_half[:], -0.5)
+
+        bias_cols = consts.tile([P, 2 * CHUNKS], F32)
+
+        def bias_to_partitions():
+            bias_rows_f = consts.tile([P, P], F32)
+            nc.vector.tensor_copy(out=bias_rows_f[:], in_=bias_rows[:])
+            bias_ps = psum.tile([P, P], F32, tag="h")
+            nc.tensor.transpose(bias_ps[:], bias_rows_f[:], ident[:])
+            nc.vector.tensor_copy(out=bias_cols[:], in_=bias_ps[:, 0 : 2 * CHUNKS])
+
+        def quantise(g):
+            main_sb, branch_sb = main_of[g], branch_of[g]
+            grouped = work.tile([P, 2, ROWS, 4], BF16, align_bytes=64)
+            grouped_words = grouped[:].bitcast(F32)
+            for j in range(GROUP):
+                xt = psum.tile([P, 2, 2, P], F32, tag="xt")
+                for x, src in enumerate((main_sb, branch_sb)):
+                    words = src[:, j, :].bitcast(F32)
+                    for u in range(2):
+                        nc.tensor.transpose(xt[:, x, u, :], words[:, u : H // 2 : 2], ident[:])
+                nc.scalar.copy(
+                    out=grouped_words[:, :, j * P : (j + 1) * P, :], in_=xt[:].rearrange("p x u r -> p x r u")
+                )
+            codes = work.tile([P, 2, ROWS], U32, align_bytes=64)
+            x_scales = work.tile([P, 2, ROWS], U8, align_bytes=64)
+            nc.vector.quantize_mx(
+                out=codes[:].rearrange("p x r -> p (x r)").bitcast(FP8X4),
+                scales=x_scales[:].rearrange("p x r -> p (x r)"),
+                in_=grouped[:].rearrange("p x r t -> p (x r t)"),
+            )
+            return codes, x_scales
+
+        def gates(g, codes, x_scales):
+            def mx_pass(acc, a, x, c, start, stop):
+                nc.tensor.matmul_mx(
+                    out=acc[:],
+                    lhsT=w_words[:, a, 2 * P * c : 2 * P * (c + 1)].bitcast(FP4X4),
+                    lhsT_scale=w_scales[:, a, P * c : P * (c + 1)],
+                    rhs=codes[:, x, :].bitcast(FP8X4),
+                    rhs_scale=x_scales[:, x, :],
+                    start=start,
+                    stop=stop,
+                )
+
+            hT = work.tile([P, CHUNKS, ROWS], F32, bufs=3)
+            for c in range(CHUNKS):
+                gate_ps = psum.tile([P, ROWS], F32, tag="gate")
+                mx_pass(gate_ps, 0, 0, c, True, False)
+                mx_pass(gate_ps, 1, 1, c, False, True)
+                value_ps = psum.tile([P, ROWS], F32, tag="value")
+                mx_pass(value_ps, 2, 1, c, True, True)
+                weight_b = work.tile([P, ROWS], F32, bufs=3)
+                nc.scalar.activation(out=weight_b[:], in_=gate_ps[:], func=ACT.Relu, bias=bias_cols[:, c : c + 1])
+                nc.vector.scalar_tensor_tensor(
+                    out=hT[:, c, :],
+                    in0=value_ps[:],
+                    scalar=bias_cols[:, CHUNKS + c : CHUNKS + c + 1],
+                    in1=weight_b[:],
+                    op0=ALU.add,
+                    op1=ALU.mult,
+                )
+            hT_of[g] = hT
+
+        def main_side(g):
+            main_sb = main_of[g]
+            em_sq = small.tile([P, GROUP], F32)
+            wm = work.tile([P, GROUP, H], F32, bufs=3)
+            for j in range(GROUP):
+                t = g * GROUP + j
+                unread_m = work.tile([P, H], BF16, tag="unread", bufs=4)
+                nc.scalar.activation(out=unread_m[:], in_=main_sb[:, j, :], func=ACT.Square, accum_out=em_sq[:, j : j + 1])
+                nc.gpsimd.tensor_scalar(
+                    out=wm[:, j, :], in0=main_sb[:, j, :], scalar1=one_minus_bag[:, t : t + 1], scalar2=0.0,
+                    op0=ALU.mult, op1=ALU.add,
+                )
+            em = small.tile([P, GROUP], F32)
+            nc.gpsimd.tensor_tensor(out=em[:], in0=em_sq[:], in1=half[:], op=ALU.pow)
+            em_of[g], wm_of[g] = em, wm
+
+        def h_rows(hT, j):
+            h_ps = psum.tile([P, H], F32, tag="h")
+            for c in range(CHUNKS):
+                nc.tensor.transpose(h_ps[:, c * P : (c + 1) * P], hT[:, c, j * P : (j + 1) * P], ident[:])
+            return h_ps
+
+        def clip_and_stats(g):
+            main_sb, hT, em = main_of[g], hT_of[g], em_of[g]
+            hm_sq = small.tile([P, GROUP], F32)
+            for j in range(GROUP):
+                h_ps = h_rows(hT, j)
+                unread_h = work.tile([P, H], BF16, tag="unread", bufs=4)
+                nc.scalar.activation(out=unread_h[:], in_=h_ps[:], func=ACT.Square, accum_out=hm_sq[:, j : j + 1])
+            hm = small.tile([P, GROUP], F32)
+            nc.gpsimd.tensor_tensor(out=hm[:], in0=hm_sq[:], in1=half[:], op=ALU.pow)
+            denom = small.tile([P, GROUP], F32)
+            nc.vector.tensor_scalar_add(out=denom[:], in0=hm[:], scalar1=BAG_EPS)
+            recip = small.tile([P, GROUP], F32)
+            nc.vector.reciprocal(out=recip[:], in_=denom[:])
+            ratio = small.tile([P, GROUP], F32)
+            nc.vector.tensor_mul(out=ratio[:], in0=recip[:], in1=em[:])
+            alpha = small.tile([P, GROUP], F32)
+            nc.vector.tensor_scalar(out=alpha[:], in0=ratio[:], scalar1=BETA_SHIFT, scalar2=1.0, op0=ALU.mult, op1=ALU.min)
+
+            pre = work.tile([P, GROUP, H], F32, bufs=3)
+            pre_sum = small.tile([P, GROUP], F32)
+            for j in range(GROUP):
+                h_ps = h_rows(hT, j)
+                nc.vector.scalar_tensor_tensor(
+                    out=pre[:, j, :], in0=h_ps[:], scalar=alpha[:, j : j + 1], in1=main_sb[:, j, :],
+                    op0=ALU.mult, op1=ALU.add, accum_out=pre_sum[:, j : j + 1],
+                )
+            negmu = small.tile([P, GROUP], F32)
+            nc.vector.tensor_scalar_mul(out=negmu[:], in0=pre_sum[:], scalar1=-1.0 / H)
+            dev_sq = small.tile([P, GROUP], F32)
+            for j in range(GROUP):
+                unread_p = work.tile([P, H], BF16, tag="unread", bufs=4)
+                nc.scalar.activation(
+                    out=unread_p[:], in_=pre[:, j, :], func=ACT.Square, bias=negmu[:, j : j + 1],
+                    accum_out=dev_sq[:, j : j + 1],
+                )
+            var_eps = small.tile([P, GROUP], F32)
+            nc.vector.tensor_scalar(out=var_eps[:], in0=dev_sq[:], scalar1=1.0 / H, scalar2=LN_EPS, op0=ALU.mult, op1=ALU.add)
+            rstd = small.tile([P, GROUP], F32)
+            nc.gpsimd.tensor_tensor(out=rstd[:], in0=var_eps[:], in1=minus_half[:], op=ALU.pow)
+            pre_of[g], negmu_of[g], rstd_of[g] = pre, negmu, rstd
+
+        def outputs(g):
+            pre, wm, negmu, rstd, o_sb = pre_of[g], wm_of[g], negmu_of[g], rstd_of[g], o_of[g]
+            for j in range(GROUP):
+                t = g * GROUP + j
+                centred = work.tile([P, H], F32, bufs=3)
+                nc.vector.scalar_tensor_tensor(
+                    out=centred[:], in0=pre[:, j, :], scalar=negmu[:, j : j + 1], in1=gain[:], op0=ALU.add, op1=ALU.mult
+                )
+                emb = work.tile([P, H], F32, bufs=3)
+                nc.vector.scalar_tensor_tensor(
+                    out=emb[:], in0=centred[:], scalar=rstd[:, j : j + 1], in1=shift[:], op0=ALU.mult, op1=ALU.add
+                )
+                shift_c = work.tile([P, H], F32, bufs=4)
+                nc.vector.scalar_tensor_tensor(
+                    out=shift_c[:], in0=emb[:], scalar=bag[:, t : t + 1], in1=wm[:, j, :], op0=ALU.mult, op1=ALU.add
+                )
+                nc.sync.dma_start(out=shift_v[:, t, :], in_=shift_c[:])
+                tanh_c = work.tile([P, H], F32, bufs=4)
+                nc.scalar.activation(out=tanh_c[:], in_=shift_c[:], func=ACT.Tanh)
+                h_sb = work.tile([P, H], F32, bufs=4)
+                nc.gpsimd.tensor_tensor(out=h_sb[:], in0=tanh_c[:], in1=o_sb[:, j, :], op=ALU.mult)
+                nc.sync.dma_start(out=h_v[:, t, :], in_=h_sb[:])
+
+        for step in range(GROUPS + 2):
+            if step + LOAD_AHEAD < GROUPS:
+                load(step + LOAD_AHEAD)
+            if step < GROUPS:
+                load_o(step)
+                codes, x_scales = quantise(step)
+                if step == 0:
+                    bias_to_partitions()
+                gates(step, codes, x_scales)
+                main_side(step)
+            if 1 <= step <= GROUPS:
+                clip_and_stats(step - 1)
+            if step >= 2:
+                outputs(step - 2)

@@ -176,7 +176,7 @@ def tile_bag_lstm_pb_t_kernel(
                 t = g * GROUP + j
                 unread_m = work.tile([P, H], BF16, tag="unread", bufs=4)
                 nc.scalar.activation(out=unread_m[:], in_=main_sb[:, j, :], func=ACT.Square, accum_out=em_sq[:, j : j + 1])
-                nc.gpsimd.tensor_scalar(
+                nc.vector.tensor_scalar(
                     out=wm[:, j, :], in0=main_sb[:, j, :], scalar1=one_minus_bag[:, t : t + 1], scalar2=0.0,
                     op0=ALU.mult, op1=ALU.add,
                 )
@@ -251,7 +251,7 @@ def tile_bag_lstm_pb_t_kernel(
                 tanh_c = work.tile([P, H], F32, bufs=4)
                 nc.scalar.activation(out=tanh_c[:], in_=shift_c[:], func=ACT.Tanh)
                 h_sb = work.tile([P, H], F32, bufs=4)
-                nc.gpsimd.tensor_tensor(out=h_sb[:], in0=tanh_c[:], in1=o_sb[:, j, :], op=ALU.mult)
+                nc.vector.tensor_tensor(out=h_sb[:], in0=tanh_c[:], in1=o_sb[:, j, :], op=ALU.mult)
                 nc.sync.dma_start(out=h_v[:, t, :], in_=h_sb[:])
 
         for step in range(GROUPS + 2):

@@ -91,10 +91,17 @@ def tile_bag_lstm_pb_t_kernel(
         for g in range(1, LOAD_AHEAD):
             load(g)
 
-        gain = consts.tile([P, H], BF16)
-        nc.scalar.dma_start(out=gain[:], in_=ln_g.partition_broadcast(P))
-        shift = consts.tile([P, H], BF16)
-        nc.scalar.dma_start(out=shift[:], in_=ln_b.partition_broadcast(P))
+        ln_rows = consts.tile([P, 2, H], BF16)
+        nc.vector.memset(ln_rows[:], 0.0)
+        nc.scalar.dma_start(out=ln_rows[0:1, 0, :], in_=ln_g.rearrange("(o f) -> o f", o=1))
+        nc.scalar.dma_start(out=ln_rows[0:1, 1, :], in_=ln_b.rearrange("(o f) -> o f", o=1))
+        ones = consts.tile([P, P], BF16)
+        nc.vector.memset(ones[:], 1.0)
+        ln_ps = psum.tile([P, 2, H], BF16, tag="ln", bufs=1)
+        nc.tensor.matmul(out=ln_ps[:, 0, :], lhsT=ones[:], rhs=ln_rows[:, 0, :], start=True, stop=True)
+        nc.tensor.matmul(out=ln_ps[:, 1, :], lhsT=ones[:], rhs=ln_rows[:, 1, :], start=True, stop=True)
+        gain = ln_ps[:, 0, :]
+        shift = ln_ps[:, 1, :]
 
         bag = consts.tile([P, TILES], F32)
         nc.vector.tensor_copy(out=bag[:], in_=bag_bf[:])
@@ -120,7 +127,7 @@ def tile_bag_lstm_pb_t_kernel(
             grouped = work.tile([P, 2, ROWS, 4], BF16, align_bytes=64)
             grouped_words = grouped[:].bitcast(F32)
             for j in range(GROUP):
-                xt = psum.tile([P, 2, 2, P], F32, tag="xt")
+                xt = psum.tile([P, 2, 2, P], F32, tag="xt", bufs=1)
                 for x, src in enumerate((main_sb, branch_sb)):
                     words = src[:, j, :].bitcast(F32)
                     for u in range(2):
@@ -176,7 +183,7 @@ def tile_bag_lstm_pb_t_kernel(
                 t = g * GROUP + j
                 unread_m = work.tile([P, H], BF16, tag="unread", bufs=4)
                 nc.scalar.activation(out=unread_m[:], in_=main_sb[:, j, :], func=ACT.Square, accum_out=em_sq[:, j : j + 1])
-                nc.vector.tensor_scalar(
+                nc.gpsimd.tensor_scalar(
                     out=wm[:, j, :], in0=main_sb[:, j, :], scalar1=one_minus_bag[:, t : t + 1], scalar2=0.0,
                     op0=ALU.mult, op1=ALU.add,
                 )
@@ -237,11 +244,11 @@ def tile_bag_lstm_pb_t_kernel(
                 t = g * GROUP + j
                 centred = work.tile([P, H], F32, bufs=3)
                 nc.vector.scalar_tensor_tensor(
-                    out=centred[:], in0=pre[:, j, :], scalar=negmu[:, j : j + 1], in1=gain[:], op0=ALU.add, op1=ALU.mult
+                    out=centred[:], in0=pre[:, j, :], scalar=negmu[:, j : j + 1], in1=gain, op0=ALU.add, op1=ALU.mult
                 )
                 emb = work.tile([P, H], F32, bufs=3)
                 nc.vector.scalar_tensor_tensor(
-                    out=emb[:], in0=centred[:], scalar=rstd[:, j : j + 1], in1=shift[:], op0=ALU.mult, op1=ALU.add
+                    out=emb[:], in0=centred[:], scalar=rstd[:, j : j + 1], in1=shift, op0=ALU.mult, op1=ALU.add
                 )
                 shift_c = work.tile([P, H], F32, bufs=4)
                 nc.vector.scalar_tensor_tensor(
@@ -251,7 +258,7 @@ def tile_bag_lstm_pb_t_kernel(
                 tanh_c = work.tile([P, H], F32, bufs=4)
                 nc.scalar.activation(out=tanh_c[:], in_=shift_c[:], func=ACT.Tanh)
                 h_sb = work.tile([P, H], F32, bufs=4)
-                nc.vector.tensor_tensor(out=h_sb[:], in0=tanh_c[:], in1=o_sb[:, j, :], op=ALU.mult)
+                nc.gpsimd.tensor_tensor(out=h_sb[:], in0=tanh_c[:], in1=o_sb[:, j, :], op=ALU.mult)
                 nc.sync.dma_start(out=h_v[:, t, :], in_=h_sb[:])
 
         for step in range(GROUPS + 2):

@@ -17,16 +17,31 @@ P = 128
 B, H = 4096, 512
 TILES = B // P
 GROUP = 4
-GROUPS = TILES // GROUP
 ROWS = GROUP * P
 CHUNKS = H // P
 PASSES = 3
 LN_EPS = 1e-5
 BAG_EPS = 1e-6
 BETA_SHIFT = 1.0
-LOAD_AHEAD = 2
 
 FLOPS = 2 * B * (2 * H + H) * H
+
+AT_LOAD = -GROUP
+AT_TURN = 0
+AT_NORM_MAIN = 2
+AT_QUANTISE = AT_TURN + GROUP - 1
+AT_MATMUL = AT_QUANTISE + 2
+AT_PRODUCT = AT_MATMUL + 1
+AT_ROOT_MAIN = AT_NORM_MAIN + GROUP
+AT_NORM_H = AT_PRODUCT + CHUNKS - 1
+AT_ALPHA = AT_NORM_H + GROUP
+AT_CLIP = AT_ALPHA + 1
+AT_DEVIATION = AT_CLIP + 1
+AT_VARIANCE = AT_DEVIATION + 2
+AT_INV_STD = AT_VARIANCE + 1
+AT_BLEND = AT_INV_STD + 1
+AT_OUT = AT_BLEND + 2
+AT_LOAD_O = AT_OUT - GROUP - 1
 
 
 def tile_bag_lstm_pb_t_kernel(
@@ -43,60 +58,51 @@ def tile_bag_lstm_pb_t_kernel(
         consts = ctx.enter_context(tc.tile_pool(name="consts", bufs=1))
         inputs = ctx.enter_context(tc.tile_pool(name="inputs", bufs=3))
         work = ctx.enter_context(tc.tile_pool(name="work", bufs=2))
-        small = ctx.enter_context(tc.tile_pool(name="small", bufs=3))
+        small = ctx.enter_context(tc.tile_pool(name="small", bufs=4))
         psum = ctx.enter_context(tc.psum_pool(name="psum", bufs=2))
+        ctx.enter_context(tc.manual_schedule())
 
-        main_of, branch_of, o_of = {}, {}, {}
-        hT_of, em_of, wm_of, pre_of, negmu_of, rstd_of = {}, {}, {}, {}, {}, {}
-
-        def load(g):
-            rows = slice(g * GROUP, (g + 1) * GROUP)
-            main_sb = inputs.tile([P, GROUP, H], BF16, tag="main", bufs=4)
-            nc.sync.dma_start(out=main_sb[:], in_=main_v[:, rows, :])
-            branch_sb = inputs.tile([P, GROUP, H], BF16, tag="branch", bufs=3)
-            nc.sync.dma_start(out=branch_sb[:], in_=branch_v[:, rows, :])
-            main_of[g], branch_of[g] = main_sb, branch_sb
-
-        def load_o(g):
-            o_sb = inputs.tile([P, GROUP, H], BF16, tag="o", bufs=3)
-            nc.sync.dma_start(out=o_sb[:], in_=o_v[:, g * GROUP : (g + 1) * GROUP, :])
-            o_of[g] = o_sb
+        held = {}
 
         bias_rows = consts.tile([P, P], BF16)
         nc.vector.memset(bias_rows[:], 0.0)
         nc.scalar.dma_start(out=bias_rows[0:CHUNKS, :], in_=b_mb.rearrange("(c p) -> c p", p=P))
         nc.scalar.dma_start(out=bias_rows[CHUNKS : 2 * CHUNKS, :], in_=b_b.rearrange("(c p) -> c p", p=P))
-        bag_bf = consts.tile([P, TILES], BF16)
-        nc.scalar.dma_start(out=bag_bf[:], in_=is_bag.rearrange("(p t) o -> p (t o)", t=TILES))
-
-        load(0)
-
-        ident = consts.tile([P, P], F32)
-        make_identity(nc, ident[:])
-
-        w_words = consts.tile([P, PASSES, 2 * H], U8, align_bytes=64)
-        nc.sync.dma_start(out=w_words[:, 0:2, :].bitcast(I32), in_=W_mb_words.rearrange("g p b -> p g b").bitcast(I32))
-        nc.sync.dma_start(out=w_words[:, 2, :].bitcast(I32), in_=W_b_words[0].bitcast(I32))
-        w_scales = consts.tile([P, PASSES, H], U8, align_bytes=64)
-        nc.vector.memset(w_scales[:].bitcast(I32), 0)
-        for quad in range(4):
-            live = slice(32 * quad, 32 * quad + 4)
-            q_rows = slice(4 * quad, 4 * quad + 4)
-            nc.sync.dma_start(
-                out=w_scales[live, 0:2, :].bitcast(I32),
-                in_=W_mb_scales[:, q_rows, :].rearrange("g q n -> q g n").bitcast(I32),
-            )
-            nc.sync.dma_start(out=w_scales[live, 2, :].bitcast(I32), in_=W_b_scales[0, q_rows, :].bitcast(I32))
-
-        for g in range(1, LOAD_AHEAD):
-            load(g)
-
         ln_rows = consts.tile([P, 2, H], BF16)
         nc.vector.memset(ln_rows[:], 0.0)
         nc.scalar.dma_start(out=ln_rows[0:1, 0, :], in_=ln_g.rearrange("(o f) -> o f", o=1))
         nc.scalar.dma_start(out=ln_rows[0:1, 1, :], in_=ln_b.rearrange("(o f) -> o f", o=1))
+        bag_bf = consts.tile([P, TILES], BF16)
+        nc.scalar.dma_start(out=bag_bf[:], in_=is_bag.rearrange("(p t) o -> p (t o)", t=TILES))
+
+        ident = consts.tile([P, P], F32)
+        make_identity(nc, ident[:])
         ones = consts.tile([P, P], BF16)
         nc.vector.memset(ones[:], 1.0)
+
+        w_scales = consts.tile([P, PASSES, H], U8, align_bytes=64)
+        nc.vector.memset(w_scales[:].bitcast(I32), 0)
+        w_words = consts.tile([P, PASSES, 2 * H], U8, align_bytes=64)
+
+        def load_weights():
+            nc.sync.dma_start(out=w_words[:, 0:2, :].bitcast(I32), in_=W_mb_words.rearrange("g p b -> p g b").bitcast(I32))
+            nc.sync.dma_start(out=w_words[:, 2, :].bitcast(I32), in_=W_b_words[0].bitcast(I32))
+            for quad in range(4):
+                live_rows = slice(32 * quad, 32 * quad + 4)
+                q_rows = slice(4 * quad, 4 * quad + 4)
+                nc.sync.dma_start(
+                    out=w_scales[live_rows, 0:2, :].bitcast(I32),
+                    in_=W_mb_scales[:, q_rows, :].rearrange("g q n -> q g n").bitcast(I32),
+                )
+                nc.sync.dma_start(out=w_scales[live_rows, 2, :].bitcast(I32), in_=W_b_scales[0, q_rows, :].bitcast(I32))
+
+        bias_rows_f = consts.tile([P, P], F32)
+        nc.vector.tensor_copy(out=bias_rows_f[:], in_=bias_rows[:])
+        bias_ps = psum.tile([P, P], F32, tag="turned", bufs=3)
+        nc.tensor.transpose(bias_ps[:], bias_rows_f[:], ident[:])
+        bias_cols = consts.tile([P, 2 * CHUNKS], F32)
+        nc.vector.tensor_copy(out=bias_cols[:], in_=bias_ps[:, 0 : 2 * CHUNKS])
+
         ln_ps = psum.tile([P, 2, H], BF16, tag="ln", bufs=1)
         nc.tensor.matmul(out=ln_ps[:, 0, :], lhsT=ones[:], rhs=ln_rows[:, 0, :], start=True, stop=True)
         nc.tensor.matmul(out=ln_ps[:, 1, :], lhsT=ones[:], rhs=ln_rows[:, 1, :], start=True, stop=True)
@@ -110,168 +116,237 @@ def tile_bag_lstm_pb_t_kernel(
 
         half = consts.tile([P, GROUP], F32)
         nc.gpsimd.memset(half[:], 0.5)
-        minus_half = consts.tile([P, GROUP], F32)
+        minus_half = consts.tile([P, 2], F32)
         nc.gpsimd.memset(minus_half[:], -0.5)
 
-        bias_cols = consts.tile([P, 2 * CHUNKS], F32)
+        def load(g):
+            rows = slice(g * GROUP, (g + 1) * GROUP)
+            main_sb = inputs.tile([P, GROUP, H], BF16, tag="main", bufs=6)
+            nc.sync.dma_start(out=main_sb[:], in_=main_v[:, rows, :])
+            branch_sb = inputs.tile([P, GROUP, H], BF16, tag="branch", bufs=3)
+            nc.sync.dma_start(out=branch_sb[:], in_=branch_v[:, rows, :])
+            held["main", g], held["branch", g] = main_sb, branch_sb
+            if g == 0:
+                load_weights()
 
-        def bias_to_partitions():
-            bias_rows_f = consts.tile([P, P], F32)
-            nc.vector.tensor_copy(out=bias_rows_f[:], in_=bias_rows[:])
-            bias_ps = psum.tile([P, P], F32, tag="h")
-            nc.tensor.transpose(bias_ps[:], bias_rows_f[:], ident[:])
-            nc.vector.tensor_copy(out=bias_cols[:], in_=bias_ps[:, 0 : 2 * CHUNKS])
+        def load_o(g):
+            o_sb = inputs.tile([P, GROUP, H], BF16, tag="o", bufs=3)
+            nc.sync.dma_start(out=o_sb[:], in_=o_v[:, g * GROUP : (g + 1) * GROUP, :])
+            held["o", g] = o_sb
+
+        def transpose_in(g, j):
+            xt = psum.tile([P, 2, 2, P], F32, tag="turned", bufs=3)
+            for x, src in enumerate((held["main", g], held["branch", g])):
+                words = src[:, j, :].bitcast(F32)
+                for u in range(2):
+                    nc.tensor.transpose(xt[:, x, u, :], words[:, u : H // 2 : 2], ident[:])
+            held["xt", g, j] = xt
+
+        def copy_in(g, j):
+            if j == 0:
+                grouped = work.tile([P, 2, ROWS, 4], BF16, align_bytes=64)
+                held["grouped", g] = grouped
+            grouped_words = held["grouped", g][:].bitcast(F32)
+            nc.scalar.copy(
+                out=grouped_words[:, :, j * P : (j + 1) * P, :], in_=held["xt", g, j][:].rearrange("p x u r -> p x r u")
+            )
 
         def quantise(g):
-            main_sb, branch_sb = main_of[g], branch_of[g]
-            grouped = work.tile([P, 2, ROWS, 4], BF16, align_bytes=64)
-            grouped_words = grouped[:].bitcast(F32)
-            for j in range(GROUP):
-                xt = psum.tile([P, 2, 2, P], F32, tag="xt", bufs=1)
-                for x, src in enumerate((main_sb, branch_sb)):
-                    words = src[:, j, :].bitcast(F32)
-                    for u in range(2):
-                        nc.tensor.transpose(xt[:, x, u, :], words[:, u : H // 2 : 2], ident[:])
-                nc.scalar.copy(
-                    out=grouped_words[:, :, j * P : (j + 1) * P, :], in_=xt[:].rearrange("p x u r -> p x r u")
-                )
             codes = work.tile([P, 2, ROWS], U32, align_bytes=64)
             x_scales = work.tile([P, 2, ROWS], U8, align_bytes=64)
             nc.vector.quantize_mx(
                 out=codes[:].rearrange("p x r -> p (x r)").bitcast(FP8X4),
                 scales=x_scales[:].rearrange("p x r -> p (x r)"),
-                in_=grouped[:].rearrange("p x r t -> p (x r t)"),
+                in_=held["grouped", g][:].rearrange("p x r t -> p (x r t)"),
             )
-            return codes, x_scales
+            held["codes", g], held["x_scales", g] = codes, x_scales
 
-        def gates(g, codes, x_scales):
-            def mx_pass(acc, a, x, c, start, stop):
-                nc.tensor.matmul_mx(
-                    out=acc[:],
-                    lhsT=w_words[:, a, 2 * P * c : 2 * P * (c + 1)].bitcast(FP4X4),
-                    lhsT_scale=w_scales[:, a, P * c : P * (c + 1)],
-                    rhs=codes[:, x, :].bitcast(FP8X4),
-                    rhs_scale=x_scales[:, x, :],
-                    start=start,
-                    stop=stop,
-                )
+        def mx_pass(acc, g, a, x, c, start, stop):
+            nc.tensor.matmul_mx(
+                out=acc[:],
+                lhsT=w_words[:, a, 2 * P * c : 2 * P * (c + 1)].bitcast(FP4X4),
+                lhsT_scale=w_scales[:, a, P * c : P * (c + 1)],
+                rhs=held["codes", g][:, x, :].bitcast(FP8X4),
+                rhs_scale=held["x_scales", g][:, x, :],
+                start=start,
+                stop=stop,
+            )
 
-            hT = work.tile([P, CHUNKS, ROWS], F32, bufs=3)
-            for c in range(CHUNKS):
-                gate_ps = psum.tile([P, ROWS], F32, tag="gate")
-                mx_pass(gate_ps, 0, 0, c, True, False)
-                mx_pass(gate_ps, 1, 1, c, False, True)
-                value_ps = psum.tile([P, ROWS], F32, tag="value")
-                mx_pass(value_ps, 2, 1, c, True, True)
-                weight_b = work.tile([P, ROWS], F32, bufs=3)
-                nc.scalar.activation(out=weight_b[:], in_=gate_ps[:], func=ACT.Relu, bias=bias_cols[:, c : c + 1])
-                nc.vector.scalar_tensor_tensor(
-                    out=hT[:, c, :],
-                    in0=value_ps[:],
-                    scalar=bias_cols[:, CHUNKS + c : CHUNKS + c + 1],
-                    in1=weight_b[:],
-                    op0=ALU.add,
-                    op1=ALU.mult,
-                )
-            hT_of[g] = hT
+        def gate_matmuls(g, c):
+            gate_ps = psum.tile([P, ROWS], F32, tag="gate")
+            mx_pass(gate_ps, g, 0, 0, c, True, False)
+            mx_pass(gate_ps, g, 1, 1, c, False, True)
+            value_ps = psum.tile([P, ROWS], F32, tag="value")
+            mx_pass(value_ps, g, 2, 1, c, True, True)
+            held["gate", g, c], held["value", g, c] = gate_ps, value_ps
 
-        def main_side(g):
-            main_sb = main_of[g]
-            em_sq = small.tile([P, GROUP], F32)
-            wm = work.tile([P, GROUP, H], F32, bufs=3)
-            for j in range(GROUP):
-                t = g * GROUP + j
-                unread_m = work.tile([P, H], BF16, tag="unread", bufs=4)
-                nc.scalar.activation(out=unread_m[:], in_=main_sb[:, j, :], func=ACT.Square, accum_out=em_sq[:, j : j + 1])
-                nc.gpsimd.tensor_scalar(
-                    out=wm[:, j, :], in0=main_sb[:, j, :], scalar1=one_minus_bag[:, t : t + 1], scalar2=0.0,
-                    op0=ALU.mult, op1=ALU.add,
-                )
+        def relu_gate(g, c):
+            weight_b = work.tile([P, ROWS], F32)
+            nc.scalar.activation(out=weight_b[:], in_=held["gate", g, c][:], func=ACT.Relu, bias=bias_cols[:, c : c + 1])
+            held["weight_b", g, c] = weight_b
+
+        def product(g, c):
+            if c == 0:
+                hT = work.tile([P, CHUNKS, ROWS], F32, bufs=3)
+                held["hT", g] = hT
+            nc.vector.scalar_tensor_tensor(
+                out=held["hT", g][:, c, :],
+                in0=held["value", g, c][:],
+                scalar=bias_cols[:, CHUNKS + c : CHUNKS + c + 1],
+                in1=held["weight_b", g, c][:],
+                op0=ALU.add,
+                op1=ALU.mult,
+            )
+
+        def norm_main(g, j):
+            if j == 0:
+                em_sq = small.tile([P, GROUP], F32)
+                held["em_sq", g] = em_sq
+            unread_m = work.tile([P, H], BF16, tag="unread", bufs=4)
+            nc.scalar.activation(
+                out=unread_m[:], in_=held["main", g][:, j, :], func=ACT.Square, accum_out=held["em_sq", g][:, j : j + 1]
+            )
+
+        def root_main(g):
             em = small.tile([P, GROUP], F32)
-            nc.gpsimd.tensor_tensor(out=em[:], in0=em_sq[:], in1=half[:], op=ALU.pow)
-            em_of[g], wm_of[g] = em, wm
+            nc.gpsimd.tensor_tensor(out=em[:], in0=held["em_sq", g][:], in1=half[:], op=ALU.pow)
+            held["em", g] = em
 
-        def h_rows(hT, j):
-            h_ps = psum.tile([P, H], F32, tag="h")
+        def kept_main(g, j):
+            t = g * GROUP + j
+            wm = work.tile([P, H], F32, bufs=7)
+            nc.gpsimd.tensor_scalar(
+                out=wm[:], in0=held["main", g][:, j, :], scalar1=one_minus_bag[:, t : t + 1], scalar2=0.0,
+                op0=ALU.mult, op1=ALU.add,
+            )
+            held["wm", g, j] = wm
+
+        def transpose_back(g, j):
+            h_ps = psum.tile([P, H], F32, tag="turned", bufs=3)
             for c in range(CHUNKS):
-                nc.tensor.transpose(h_ps[:, c * P : (c + 1) * P], hT[:, c, j * P : (j + 1) * P], ident[:])
-            return h_ps
+                nc.tensor.transpose(h_ps[:, c * P : (c + 1) * P], held["hT", g][:, c, j * P : (j + 1) * P], ident[:])
+            held["h", g, j] = h_ps
 
-        def clip_and_stats(g):
-            main_sb, hT, em = main_of[g], hT_of[g], em_of[g]
-            hm_sq = small.tile([P, GROUP], F32)
-            for j in range(GROUP):
-                h_ps = h_rows(hT, j)
-                unread_h = work.tile([P, H], BF16, tag="unread", bufs=4)
-                nc.scalar.activation(out=unread_h[:], in_=h_ps[:], func=ACT.Square, accum_out=hm_sq[:, j : j + 1])
+        def norm_h(g, j):
+            if j == 0:
+                hm_sq = small.tile([P, GROUP], F32)
+                held["hm_sq", g] = hm_sq
+            unread_h = work.tile([P, H], BF16, tag="unread", bufs=4)
+            nc.scalar.activation(
+                out=unread_h[:], in_=held["h", g, j][:], func=ACT.Square, accum_out=held["hm_sq", g][:, j : j + 1]
+            )
+
+        def root_h(g):
             hm = small.tile([P, GROUP], F32)
-            nc.gpsimd.tensor_tensor(out=hm[:], in0=hm_sq[:], in1=half[:], op=ALU.pow)
+            nc.gpsimd.tensor_tensor(out=hm[:], in0=held["hm_sq", g][:], in1=half[:], op=ALU.pow)
+            held["hm", g] = hm
+
+        def clip_factor(g):
             denom = small.tile([P, GROUP], F32)
-            nc.vector.tensor_scalar_add(out=denom[:], in0=hm[:], scalar1=BAG_EPS)
+            nc.vector.tensor_scalar_add(out=denom[:], in0=held["hm", g][:], scalar1=BAG_EPS)
             recip = small.tile([P, GROUP], F32)
             nc.vector.reciprocal(out=recip[:], in_=denom[:])
             ratio = small.tile([P, GROUP], F32)
-            nc.vector.tensor_mul(out=ratio[:], in0=recip[:], in1=em[:])
+            nc.vector.tensor_mul(out=ratio[:], in0=recip[:], in1=held["em", g][:])
             alpha = small.tile([P, GROUP], F32)
             nc.vector.tensor_scalar(out=alpha[:], in0=ratio[:], scalar1=BETA_SHIFT, scalar2=1.0, op0=ALU.mult, op1=ALU.min)
+            held["alpha", g] = alpha
 
-            pre = work.tile([P, GROUP, H], F32, bufs=3)
-            pre_sum = small.tile([P, GROUP], F32)
-            for j in range(GROUP):
-                h_ps = h_rows(hT, j)
-                nc.vector.scalar_tensor_tensor(
-                    out=pre[:, j, :], in0=h_ps[:], scalar=alpha[:, j : j + 1], in1=main_sb[:, j, :],
-                    op0=ALU.mult, op1=ALU.add, accum_out=pre_sum[:, j : j + 1],
-                )
-            negmu = small.tile([P, GROUP], F32)
+        def clip(g, j):
+            pre = work.tile([P, H], F32, bufs=3)
+            pre_sum = small.tile([P, 1], F32)
+            nc.vector.scalar_tensor_tensor(
+                out=pre[:], in0=held["h", g, j][:], scalar=held["alpha", g][:, j : j + 1], in1=held["main", g][:, j, :],
+                op0=ALU.mult, op1=ALU.add, accum_out=pre_sum[:],
+            )
+            negmu = small.tile([P, 1], F32)
             nc.vector.tensor_scalar_mul(out=negmu[:], in0=pre_sum[:], scalar1=-1.0 / H)
-            dev_sq = small.tile([P, GROUP], F32)
-            for j in range(GROUP):
-                unread_p = work.tile([P, H], BF16, tag="unread", bufs=4)
-                nc.scalar.activation(
-                    out=unread_p[:], in_=pre[:, j, :], func=ACT.Square, bias=negmu[:, j : j + 1],
-                    accum_out=dev_sq[:, j : j + 1],
-                )
-            var_eps = small.tile([P, GROUP], F32)
-            nc.vector.tensor_scalar(out=var_eps[:], in0=dev_sq[:], scalar1=1.0 / H, scalar2=LN_EPS, op0=ALU.mult, op1=ALU.add)
-            rstd = small.tile([P, GROUP], F32)
-            nc.gpsimd.tensor_tensor(out=rstd[:], in0=var_eps[:], in1=minus_half[:], op=ALU.pow)
-            pre_of[g], negmu_of[g], rstd_of[g] = pre, negmu, rstd
+            centred = work.tile([P, H], F32, bufs=7)
+            nc.vector.scalar_tensor_tensor(out=centred[:], in0=pre[:], scalar=negmu[:], in1=gain, op0=ALU.add, op1=ALU.mult)
+            held["pre", g, j], held["negmu", g, j], held["centred", g, j] = pre, negmu, centred
 
-        def outputs(g):
-            pre, wm, negmu, rstd, o_sb = pre_of[g], wm_of[g], negmu_of[g], rstd_of[g], o_of[g]
-            for j in range(GROUP):
-                t = g * GROUP + j
-                centred = work.tile([P, H], F32, bufs=3)
-                nc.vector.scalar_tensor_tensor(
-                    out=centred[:], in0=pre[:, j, :], scalar=negmu[:, j : j + 1], in1=gain, op0=ALU.add, op1=ALU.mult
-                )
-                emb = work.tile([P, H], F32, bufs=3)
-                nc.vector.scalar_tensor_tensor(
-                    out=emb[:], in0=centred[:], scalar=rstd[:, j : j + 1], in1=shift, op0=ALU.mult, op1=ALU.add
-                )
-                shift_c = work.tile([P, H], F32, bufs=4)
-                nc.vector.scalar_tensor_tensor(
-                    out=shift_c[:], in0=emb[:], scalar=bag[:, t : t + 1], in1=wm[:, j, :], op0=ALU.mult, op1=ALU.add
-                )
-                nc.sync.dma_start(out=shift_v[:, t, :], in_=shift_c[:])
-                tanh_c = work.tile([P, H], F32, bufs=4)
-                nc.scalar.activation(out=tanh_c[:], in_=shift_c[:], func=ACT.Tanh)
-                h_sb = work.tile([P, H], F32, bufs=4)
-                nc.gpsimd.tensor_tensor(out=h_sb[:], in0=tanh_c[:], in1=o_sb[:, j, :], op=ALU.mult)
-                nc.sync.dma_start(out=h_v[:, t, :], in_=h_sb[:])
+        def deviation(g, j):
+            if j % 2 == 0:
+                dev_sq = small.tile([P, 2], F32)
+                held["dev_sq", g, j // 2] = dev_sq
+            unread_p = work.tile([P, H], BF16, tag="unread", bufs=4)
+            nc.scalar.activation(
+                out=unread_p[:], in_=held["pre", g, j][:], func=ACT.Square, bias=held["negmu", g, j][:],
+                accum_out=held["dev_sq", g, j // 2][:, j % 2 : j % 2 + 1],
+            )
 
-        for step in range(GROUPS + 2):
-            if step + LOAD_AHEAD < GROUPS:
-                load(step + LOAD_AHEAD)
-            if step < GROUPS:
-                load_o(step)
-                codes, x_scales = quantise(step)
-                if step == 0:
-                    bias_to_partitions()
-                gates(step, codes, x_scales)
-                main_side(step)
-            if 1 <= step <= GROUPS:
-                clip_and_stats(step - 1)
-            if step >= 2:
-                outputs(step - 2)
+        def variance(g, pair):
+            var_eps = small.tile([P, 2], F32)
+            nc.vector.tensor_scalar(
+                out=var_eps[:], in0=held["dev_sq", g, pair][:], scalar1=1.0 / H, scalar2=LN_EPS, op0=ALU.mult, op1=ALU.add
+            )
+            held["var_eps", g, pair] = var_eps
+
+        def inv_std(g, pair):
+            rstd = small.tile([P, 2], F32)
+            nc.gpsimd.tensor_tensor(out=rstd[:], in0=held["var_eps", g, pair][:], in1=minus_half[:], op=ALU.pow)
+            held["rstd", g, pair] = rstd
+
+        def blend(g, j):
+            t = g * GROUP + j
+            emb = work.tile([P, H], F32, bufs=3)
+            nc.vector.scalar_tensor_tensor(
+                out=emb[:], in0=held["centred", g, j][:], scalar=held["rstd", g, j // 2][:, j % 2 : j % 2 + 1], in1=shift,
+                op0=ALU.mult, op1=ALU.add,
+            )
+            shift_c = work.tile([P, H], F32, bufs=4)
+            nc.vector.scalar_tensor_tensor(
+                out=shift_c[:], in0=emb[:], scalar=bag[:, t : t + 1], in1=held["wm", g, j][:], op0=ALU.mult, op1=ALU.add
+            )
+            nc.sync.dma_start(out=shift_v[:, t, :], in_=shift_c[:])
+            held["shift_c", g, j] = shift_c
+
+        def squash(g, j):
+            tanh_c = work.tile([P, H], F32, bufs=3)
+            nc.scalar.activation(out=tanh_c[:], in_=held["shift_c", g, j][:], func=ACT.Tanh)
+            held["tanh_c", g, j] = tanh_c
+
+        def gate_out(g, j):
+            h_sb = work.tile([P, H], F32, bufs=3)
+            nc.gpsimd.tensor_tensor(out=h_sb[:], in0=held["tanh_c", g, j][:], in1=held["o", g][:, j, :], op=ALU.mult)
+            nc.sync.dma_start(out=h_v[:, g * GROUP + j, :], in_=h_sb[:])
+
+        def per_tile(step, lag, stage):
+            t = step - lag
+            if 0 <= t < TILES:
+                stage(t // GROUP, t % GROUP)
+
+        def per_pair(step, lag, stage):
+            t = step - lag
+            if 0 <= t < TILES and t % 2 == 0:
+                stage(t // GROUP, (t % GROUP) // 2)
+
+        def per_group(step, lag, stage):
+            t = step - lag
+            if 0 <= t < TILES and t % GROUP == 0:
+                stage(t // GROUP)
+
+        for step in range(AT_LOAD, TILES + AT_OUT):
+            per_group(step, AT_LOAD, load)
+            per_group(step, AT_LOAD_O, load_o)
+            per_tile(step, AT_OUT, squash)
+            per_pair(step, AT_INV_STD, inv_std)
+            per_group(step, AT_ALPHA, root_h)
+            per_group(step, AT_ROOT_MAIN, root_main)
+            per_tile(step, AT_OUT, gate_out)
+            per_tile(step, AT_CLIP, kept_main)
+            per_tile(step, AT_PRODUCT, product)
+            per_tile(step, AT_CLIP, clip)
+            per_tile(step, AT_TURN, transpose_in)
+            per_tile(step, AT_MATMUL, gate_matmuls)
+            per_tile(step, AT_NORM_H, transpose_back)
+            per_tile(step, AT_CLIP - 1, transpose_back)
+            per_tile(step, AT_BLEND, blend)
+            per_tile(step, AT_NORM_MAIN, norm_main)
+            per_tile(step, AT_TURN, copy_in)
+            per_tile(step, AT_MATMUL, relu_gate)
+            per_tile(step, AT_DEVIATION, deviation)
+            per_tile(step, AT_NORM_H, norm_h)
+            per_pair(step, AT_VARIANCE, variance)
+            per_group(step, AT_ALPHA, clip_factor)
+            per_group(step, AT_QUANTISE, quantise)

@@ -16,32 +16,34 @@ ACT = mybir.ActivationFunctionType
 P = 128
 B, H = 4096, 512
 TILES = B // P
-GROUP = 4
+GROUP = 2
 ROWS = GROUP * P
 CHUNKS = H // P
+SHARE = CHUNKS // GROUP
+LOAD = 4
+LOADS = [0, 1, 2] + list(range(4, TILES + 1, LOAD))
 PASSES = 3
 LN_EPS = 1e-5
 BAG_EPS = 1e-6
-BETA_SHIFT = 1.0
 
 FLOPS = 2 * B * (2 * H + H) * H
 
-AT_LOAD = -GROUP
 AT_TURN = 0
-AT_NORM_MAIN = 2
 AT_QUANTISE = AT_TURN + GROUP - 1
-AT_MATMUL = AT_QUANTISE + 2
+AT_NORM_MAIN = 2
+AT_MATMUL = AT_QUANTISE + 1
 AT_PRODUCT = AT_MATMUL + 1
-AT_ROOT_MAIN = AT_NORM_MAIN + GROUP
-AT_NORM_H = AT_PRODUCT + CHUNKS - 1
+AT_NORM_H = AT_PRODUCT + GROUP - 1
 AT_ALPHA = AT_NORM_H + GROUP
-AT_CLIP = AT_ALPHA + 1
+AT_CLIP = AT_ALPHA
 AT_DEVIATION = AT_CLIP + 1
-AT_VARIANCE = AT_DEVIATION + 2
-AT_INV_STD = AT_VARIANCE + 1
-AT_BLEND = AT_INV_STD + 1
+AT_CENTRE = AT_DEVIATION + 1
+AT_VARIANCE = AT_DEVIATION + GROUP
+AT_EMB = AT_VARIANCE
+AT_BLEND = AT_EMB + 1
 AT_OUT = AT_BLEND + 2
-AT_LOAD_O = AT_OUT - GROUP - 1
+LOAD_AHEAD = 6
+LOAD_O_AHEAD = 5
 
 
 def tile_bag_lstm_pb_t_kernel(
@@ -64,25 +66,29 @@ def tile_bag_lstm_pb_t_kernel(
 
         held = {}
 
-        bias_rows = consts.tile([P, P], BF16)
-        nc.vector.memset(bias_rows[:], 0.0)
-        nc.scalar.dma_start(out=bias_rows[0:CHUNKS, :], in_=b_mb.rearrange("(c p) -> c p", p=P))
-        nc.scalar.dma_start(out=bias_rows[CHUNKS : 2 * CHUNKS, :], in_=b_b.rearrange("(c p) -> c p", p=P))
-        ln_rows = consts.tile([P, 2, H], BF16)
-        nc.vector.memset(ln_rows[:], 0.0)
-        nc.scalar.dma_start(out=ln_rows[0:1, 0, :], in_=ln_g.rearrange("(o f) -> o f", o=1))
-        nc.scalar.dma_start(out=ln_rows[0:1, 1, :], in_=ln_b.rearrange("(o f) -> o f", o=1))
-        bag_bf = consts.tile([P, TILES], BF16)
-        nc.scalar.dma_start(out=bag_bf[:], in_=is_bag.rearrange("(p t) o -> p (t o)", t=TILES))
-
         ident = consts.tile([P, P], F32)
         make_identity(nc, ident[:])
-        ones = consts.tile([P, P], BF16)
-        nc.vector.memset(ones[:], 1.0)
-
         w_scales = consts.tile([P, PASSES, H], U8, align_bytes=64)
         nc.vector.memset(w_scales[:].bitcast(I32), 0)
+        bias_rows = consts.tile([P, P], BF16)
+        nc.vector.memset(bias_rows[:], 0.0)
+        ln_rows = consts.tile([P, 2, H], BF16)
+        nc.vector.memset(ln_rows[:], 0.0)
+        ones = consts.tile([P, P], BF16)
+        nc.vector.memset(ones[:], 1.0)
+        bag_bf = consts.tile([P, TILES], BF16)
         w_words = consts.tile([P, PASSES, 2 * H], U8, align_bytes=64)
+        half = consts.tile([P, 2, GROUP], F32)
+        nc.gpsimd.memset(half[:], 0.5)
+        minus_half = consts.tile([P, GROUP], F32)
+        nc.gpsimd.memset(minus_half[:], -0.5)
+        bias_cols = consts.tile([P, 2 * CHUNKS], F32)
+        ln_ps = psum.tile([P, 2, H], BF16, tag="ln", bufs=1)
+        gain = ln_ps[:, 0, :]
+        shift = ln_ps[:, 1, :]
+        bag = consts.tile([P, TILES], F32)
+        one_minus_bag = consts.tile([P, TILES], F32)
+        bias_rows_f = consts.tile([P, P], F32)
 
         def load_weights():
             nc.sync.dma_start(out=w_words[:, 0:2, :].bitcast(I32), in_=W_mb_words.rearrange("g p b -> p g b").bitcast(I32))
@@ -95,49 +101,52 @@ def tile_bag_lstm_pb_t_kernel(
                     in_=W_mb_scales[:, q_rows, :].rearrange("g q n -> q g n").bitcast(I32),
                 )
                 nc.sync.dma_start(out=w_scales[live_rows, 2, :].bitcast(I32), in_=W_b_scales[0, q_rows, :].bitcast(I32))
+            nc.sync.dma_start(out=bias_rows[0:CHUNKS, :], in_=b_mb.rearrange("(c p) -> c p", p=P))
+            nc.sync.dma_start(out=bias_rows[CHUNKS : 2 * CHUNKS, :], in_=b_b.rearrange("(c p) -> c p", p=P))
+            nc.sync.dma_start(out=bag_bf[:], in_=is_bag.rearrange("(p t) o -> p (t o)", t=TILES))
 
-        bias_rows_f = consts.tile([P, P], F32)
-        nc.vector.tensor_copy(out=bias_rows_f[:], in_=bias_rows[:])
-        bias_ps = psum.tile([P, P], F32, tag="turned", bufs=3)
-        nc.tensor.transpose(bias_ps[:], bias_rows_f[:], ident[:])
-        bias_cols = consts.tile([P, 2 * CHUNKS], F32)
-        nc.vector.tensor_copy(out=bias_cols[:], in_=bias_ps[:, 0 : 2 * CHUNKS])
+        def load_vectors():
+            nc.sync.dma_start(out=ln_rows[0:1, 0, :], in_=ln_g.rearrange("(o f) -> o f", o=1))
+            nc.sync.dma_start(out=ln_rows[0:1, 1, :], in_=ln_b.rearrange("(o f) -> o f", o=1))
 
-        ln_ps = psum.tile([P, 2, H], BF16, tag="ln", bufs=1)
-        nc.tensor.matmul(out=ln_ps[:, 0, :], lhsT=ones[:], rhs=ln_rows[:, 0, :], start=True, stop=True)
-        nc.tensor.matmul(out=ln_ps[:, 1, :], lhsT=ones[:], rhs=ln_rows[:, 1, :], start=True, stop=True)
-        gain = ln_ps[:, 0, :]
-        shift = ln_ps[:, 1, :]
+        def prepare_biases():
+            nc.vector.tensor_copy(out=bias_rows_f[:], in_=bias_rows[:])
+            bias_ps = psum.tile([P, P], F32, tag="turned", bufs=3)
+            nc.tensor.transpose(bias_ps[:], bias_rows_f[:], ident[:])
+            nc.vector.tensor_copy(out=bias_cols[:], in_=bias_ps[:, 0 : 2 * CHUNKS])
 
-        bag = consts.tile([P, TILES], F32)
-        nc.vector.tensor_copy(out=bag[:], in_=bag_bf[:])
-        one_minus_bag = consts.tile([P, TILES], F32)
-        nc.vector.tensor_scalar(out=one_minus_bag[:], in0=bag[:], scalar1=-1.0, scalar2=1.0, op0=ALU.mult, op1=ALU.add)
+        def prepare_bag():
+            nc.vector.tensor_copy(out=bag[:], in_=bag_bf[:])
+            nc.vector.tensor_scalar(
+                out=one_minus_bag[:], in0=bag[:], scalar1=-1.0, scalar2=1.0, op0=ALU.mult, op1=ALU.add
+            )
 
-        half = consts.tile([P, GROUP], F32)
-        nc.gpsimd.memset(half[:], 0.5)
-        minus_half = consts.tile([P, 2], F32)
-        nc.gpsimd.memset(minus_half[:], -0.5)
+        def prepare_vectors():
+            nc.tensor.matmul(out=gain, lhsT=ones[:], rhs=ln_rows[:, 0, :], start=True, stop=True)
+            nc.tensor.matmul(out=shift, lhsT=ones[:], rhs=ln_rows[:, 1, :], start=True, stop=True)
 
-        def load(g):
-            rows = slice(g * GROUP, (g + 1) * GROUP)
-            main_sb = inputs.tile([P, GROUP, H], BF16, tag="main", bufs=6)
-            nc.sync.dma_start(out=main_sb[:], in_=main_v[:, rows, :])
-            branch_sb = inputs.tile([P, GROUP, H], BF16, tag="branch", bufs=3)
-            nc.sync.dma_start(out=branch_sb[:], in_=branch_v[:, rows, :])
-            held["main", g], held["branch", g] = main_sb, branch_sb
-            if g == 0:
-                load_weights()
+        def load(b):
+            first, end = LOADS[b], LOADS[b + 1]
+            main_sb = inputs.tile([P, LOAD, H], BF16, tag="main", bufs=6)
+            nc.sync.dma_start(out=main_sb[:, 0 : end - first, :], in_=main_v[:, first:end, :])
+            branch_sb = inputs.tile([P, LOAD, H], BF16, tag="branch", bufs=4)
+            nc.sync.dma_start(out=branch_sb[:, 0 : end - first, :], in_=branch_v[:, first:end, :])
+            for t in range(first, end):
+                held["main", t], held["branch", t] = main_sb[:, t - first, :], branch_sb[:, t - first, :]
 
-        def load_o(g):
-            o_sb = inputs.tile([P, GROUP, H], BF16, tag="o", bufs=3)
-            nc.sync.dma_start(out=o_sb[:], in_=o_v[:, g * GROUP : (g + 1) * GROUP, :])
-            held["o", g] = o_sb
+        def load_o(b):
+            o_sb = inputs.tile([P, LOAD, H], BF16, tag="o", bufs=3)
+            nc.sync.dma_start(out=o_sb[:], in_=o_v[:, b * LOAD : (b + 1) * LOAD, :])
+            for i in range(LOAD):
+                held["o", b * LOAD + i] = o_sb[:, i, :]
+
+        def rows_of(name, g, j):
+            return held[name, g * GROUP + j]
 
         def transpose_in(g, j):
             xt = psum.tile([P, 2, 2, P], F32, tag="turned", bufs=3)
-            for x, src in enumerate((held["main", g], held["branch", g])):
-                words = src[:, j, :].bitcast(F32)
+            for x, name in enumerate(("main", "branch")):
+                words = rows_of(name, g, j).bitcast(F32)
                 for u in range(2):
                     nc.tensor.transpose(xt[:, x, u, :], words[:, u : H // 2 : 2], ident[:])
             held["xt", g, j] = xt
@@ -161,62 +170,67 @@ def tile_bag_lstm_pb_t_kernel(
             )
             held["codes", g], held["x_scales", g] = codes, x_scales
 
-        def mx_pass(acc, g, a, x, c, start, stop):
+        def mx_pass(acc, g, a, x, c, rows, start, stop):
             nc.tensor.matmul_mx(
-                out=acc[:],
+                out=acc[:, rows],
                 lhsT=w_words[:, a, 2 * P * c : 2 * P * (c + 1)].bitcast(FP4X4),
                 lhsT_scale=w_scales[:, a, P * c : P * (c + 1)],
-                rhs=held["codes", g][:, x, :].bitcast(FP8X4),
-                rhs_scale=held["x_scales", g][:, x, :],
+                rhs=held["codes", g][:, x, rows].bitcast(FP8X4),
+                rhs_scale=held["x_scales", g][:, x, rows],
                 start=start,
                 stop=stop,
             )
 
-        def gate_matmuls(g, c):
-            gate_ps = psum.tile([P, ROWS], F32, tag="gate")
-            mx_pass(gate_ps, g, 0, 0, c, True, False)
-            mx_pass(gate_ps, g, 1, 1, c, False, True)
-            value_ps = psum.tile([P, ROWS], F32, tag="value")
-            mx_pass(value_ps, g, 2, 1, c, True, True)
-            held["gate", g, c], held["value", g, c] = gate_ps, value_ps
+        def gate_matmuls(g, s):
+            gate_ps = psum.tile([P, SHARE, ROWS], F32, tag="gate")
+            value_ps = psum.tile([P, SHARE, ROWS], F32, tag="value")
+            for i in range(SHARE):
+                for j in range(GROUP):
+                    rows = slice(j * P, (j + 1) * P)
+                    mx_pass(gate_ps[:, i, :], g, 0, 0, SHARE * s + i, rows, True, False)
+                    mx_pass(gate_ps[:, i, :], g, 1, 1, SHARE * s + i, rows, False, True)
+            for i in range(SHARE):
+                mx_pass(value_ps[:, i, :], g, 2, 1, SHARE * s + i, slice(0, ROWS), True, True)
+            held["gate", g, s], held["value", g, s] = gate_ps, value_ps
 
-        def relu_gate(g, c):
-            weight_b = work.tile([P, ROWS], F32)
-            nc.scalar.activation(out=weight_b[:], in_=held["gate", g, c][:], func=ACT.Relu, bias=bias_cols[:, c : c + 1])
-            held["weight_b", g, c] = weight_b
+        def relu_gate(g, s):
+            weight_b = work.tile([P, SHARE, ROWS], F32)
+            for i in range(SHARE):
+                c = SHARE * s + i
+                nc.scalar.activation(
+                    out=weight_b[:, i, :], in_=held["gate", g, s][:, i, :], func=ACT.Relu, bias=bias_cols[:, c : c + 1]
+                )
+            held["weight_b", g, s] = weight_b
 
-        def product(g, c):
-            if c == 0:
+        def product(g, s):
+            if s == 0:
                 hT = work.tile([P, CHUNKS, ROWS], F32, bufs=3)
                 held["hT", g] = hT
-            nc.vector.scalar_tensor_tensor(
-                out=held["hT", g][:, c, :],
-                in0=held["value", g, c][:],
-                scalar=bias_cols[:, CHUNKS + c : CHUNKS + c + 1],
-                in1=held["weight_b", g, c][:],
-                op0=ALU.add,
-                op1=ALU.mult,
-            )
+            for i in range(SHARE):
+                c = SHARE * s + i
+                nc.vector.scalar_tensor_tensor(
+                    out=held["hT", g][:, c, :],
+                    in0=held["value", g, s][:, i, :],
+                    scalar=bias_cols[:, CHUNKS + c : CHUNKS + c + 1],
+                    in1=held["weight_b", g, s][:, i, :],
+                    op0=ALU.add,
+                    op1=ALU.mult,
+                )
 
         def norm_main(g, j):
             if j == 0:
-                em_sq = small.tile([P, GROUP], F32)
-                held["em_sq", g] = em_sq
+                norm_sq = small.tile([P, 2, GROUP], F32)
+                held["norm_sq", g] = norm_sq
             unread_m = work.tile([P, H], BF16, tag="unread", bufs=4)
             nc.scalar.activation(
-                out=unread_m[:], in_=held["main", g][:, j, :], func=ACT.Square, accum_out=held["em_sq", g][:, j : j + 1]
+                out=unread_m[:], in_=rows_of("main", g, j), func=ACT.Square, accum_out=held["norm_sq", g][:, 0, j : j + 1]
             )
-
-        def root_main(g):
-            em = small.tile([P, GROUP], F32)
-            nc.gpsimd.tensor_tensor(out=em[:], in0=held["em_sq", g][:], in1=half[:], op=ALU.pow)
-            held["em", g] = em
 
         def kept_main(g, j):
             t = g * GROUP + j
-            wm = work.tile([P, H], F32, bufs=7)
+            wm = work.tile([P, H], F32, bufs=12)
             nc.gpsimd.tensor_scalar(
-                out=wm[:], in0=held["main", g][:, j, :], scalar1=one_minus_bag[:, t : t + 1], scalar2=0.0,
+                out=wm[:], in0=rows_of("main", g, j), scalar1=one_minus_bag[:, t : t + 1], scalar2=0.0,
                 op0=ALU.mult, op1=ALU.add,
             )
             held["wm", g, j] = wm
@@ -228,75 +242,83 @@ def tile_bag_lstm_pb_t_kernel(
             held["h", g, j] = h_ps
 
         def norm_h(g, j):
-            if j == 0:
-                hm_sq = small.tile([P, GROUP], F32)
-                held["hm_sq", g] = hm_sq
             unread_h = work.tile([P, H], BF16, tag="unread", bufs=4)
             nc.scalar.activation(
-                out=unread_h[:], in_=held["h", g, j][:], func=ACT.Square, accum_out=held["hm_sq", g][:, j : j + 1]
+                out=unread_h[:], in_=held["h", g, j][:], func=ACT.Square, accum_out=held["norm_sq", g][:, 1, j : j + 1]
             )
 
-        def root_h(g):
-            hm = small.tile([P, GROUP], F32)
-            nc.gpsimd.tensor_tensor(out=hm[:], in0=held["hm_sq", g][:], in1=half[:], op=ALU.pow)
-            held["hm", g] = hm
+        def roots(g):
+            norms = small.tile([P, 2, GROUP], F32)
+            nc.gpsimd.tensor_tensor(out=norms[:], in0=held["norm_sq", g][:], in1=half[:], op=ALU.pow)
+            held["norms", g] = norms
 
         def clip_factor(g):
+            em, hm = held["norms", g][:, 0, :], held["norms", g][:, 1, :]
             denom = small.tile([P, GROUP], F32)
-            nc.vector.tensor_scalar_add(out=denom[:], in0=held["hm", g][:], scalar1=BAG_EPS)
+            nc.vector.scalar_tensor_tensor(out=denom[:], in0=hm, scalar=BAG_EPS, in1=em, op0=ALU.add, op1=ALU.max)
             recip = small.tile([P, GROUP], F32)
             nc.vector.reciprocal(out=recip[:], in_=denom[:])
-            ratio = small.tile([P, GROUP], F32)
-            nc.vector.tensor_mul(out=ratio[:], in0=recip[:], in1=held["em", g][:])
             alpha = small.tile([P, GROUP], F32)
-            nc.vector.tensor_scalar(out=alpha[:], in0=ratio[:], scalar1=BETA_SHIFT, scalar2=1.0, op0=ALU.mult, op1=ALU.min)
+            nc.vector.tensor_mul(out=alpha[:], in0=recip[:], in1=em)
             held["alpha", g] = alpha
 
         def clip(g, j):
             pre = work.tile([P, H], F32, bufs=3)
             pre_sum = small.tile([P, 1], F32)
             nc.vector.scalar_tensor_tensor(
-                out=pre[:], in0=held["h", g, j][:], scalar=held["alpha", g][:, j : j + 1], in1=held["main", g][:, j, :],
+                out=pre[:], in0=held["h", g, j][:], scalar=held["alpha", g][:, j : j + 1], in1=rows_of("main", g, j),
                 op0=ALU.mult, op1=ALU.add, accum_out=pre_sum[:],
             )
+            held["pre", g, j], held["pre_sum", g, j] = pre, pre_sum
+
+        def mean(g, j):
             negmu = small.tile([P, 1], F32)
-            nc.vector.tensor_scalar_mul(out=negmu[:], in0=pre_sum[:], scalar1=-1.0 / H)
-            centred = work.tile([P, H], F32, bufs=7)
-            nc.vector.scalar_tensor_tensor(out=centred[:], in0=pre[:], scalar=negmu[:], in1=gain, op0=ALU.add, op1=ALU.mult)
-            held["pre", g, j], held["negmu", g, j], held["centred", g, j] = pre, negmu, centred
+            nc.vector.tensor_scalar_mul(out=negmu[:], in0=held["pre_sum", g, j][:], scalar1=-1.0 / H)
+            held["negmu", g, j] = negmu
+
+        def centre(g, j):
+            centred = work.tile([P, H], F32, bufs=3)
+            nc.vector.scalar_tensor_tensor(
+                out=centred[:], in0=held["pre", g, j][:], scalar=held["negmu", g, j][:], in1=gain, op0=ALU.add, op1=ALU.mult
+            )
+            held["centred", g, j] = centred
 
         def deviation(g, j):
-            if j % 2 == 0:
-                dev_sq = small.tile([P, 2], F32)
-                held["dev_sq", g, j // 2] = dev_sq
+            if j == 0:
+                dev_sq = small.tile([P, GROUP], F32)
+                held["dev_sq", g] = dev_sq
             unread_p = work.tile([P, H], BF16, tag="unread", bufs=4)
             nc.scalar.activation(
                 out=unread_p[:], in_=held["pre", g, j][:], func=ACT.Square, bias=held["negmu", g, j][:],
-                accum_out=held["dev_sq", g, j // 2][:, j % 2 : j % 2 + 1],
+                accum_out=held["dev_sq", g][:, j : j + 1],
             )
 
-        def variance(g, pair):
-            var_eps = small.tile([P, 2], F32)
+        def variance(g):
+            var_eps = small.tile([P, GROUP], F32)
             nc.vector.tensor_scalar(
-                out=var_eps[:], in0=held["dev_sq", g, pair][:], scalar1=1.0 / H, scalar2=LN_EPS, op0=ALU.mult, op1=ALU.add
+                out=var_eps[:], in0=held["dev_sq", g][:], scalar1=1.0 / H, scalar2=LN_EPS, op0=ALU.mult, op1=ALU.add
             )
-            held["var_eps", g, pair] = var_eps
+            held["var_eps", g] = var_eps
 
-        def inv_std(g, pair):
-            rstd = small.tile([P, 2], F32)
-            nc.gpsimd.tensor_tensor(out=rstd[:], in0=held["var_eps", g, pair][:], in1=minus_half[:], op=ALU.pow)
-            held["rstd", g, pair] = rstd
+        def inv_std(g):
+            rstd = small.tile([P, GROUP], F32)
+            nc.gpsimd.tensor_tensor(out=rstd[:], in0=held["var_eps", g][:], in1=minus_half[:], op=ALU.pow)
+            held["rstd", g] = rstd
+
+        def emb(g, j):
+            emb = work.tile([P, H], F32, bufs=3)
+            nc.vector.scalar_tensor_tensor(
+                out=emb[:], in0=held["centred", g, j][:], scalar=held["rstd", g][:, j : j + 1], in1=shift,
+                op0=ALU.mult, op1=ALU.add,
+            )
+            held["emb", g, j] = emb
 
         def blend(g, j):
             t = g * GROUP + j
-            emb = work.tile([P, H], F32, bufs=3)
+            shift_c = work.tile([P, H], F32, bufs=5)
             nc.vector.scalar_tensor_tensor(
-                out=emb[:], in0=held["centred", g, j][:], scalar=held["rstd", g, j // 2][:, j % 2 : j % 2 + 1], in1=shift,
+                out=shift_c[:], in0=held["emb", g, j][:], scalar=bag[:, t : t + 1], in1=held["wm", g, j][:],
                 op0=ALU.mult, op1=ALU.add,
-            )
-            shift_c = work.tile([P, H], F32, bufs=4)
-            nc.vector.scalar_tensor_tensor(
-                out=shift_c[:], in0=emb[:], scalar=bag[:, t : t + 1], in1=held["wm", g, j][:], op0=ALU.mult, op1=ALU.add
             )
             nc.sync.dma_start(out=shift_v[:, t, :], in_=shift_c[:])
             held["shift_c", g, j] = shift_c
@@ -308,45 +330,56 @@ def tile_bag_lstm_pb_t_kernel(
 
         def gate_out(g, j):
             h_sb = work.tile([P, H], F32, bufs=3)
-            nc.gpsimd.tensor_tensor(out=h_sb[:], in0=held["tanh_c", g, j][:], in1=held["o", g][:, j, :], op=ALU.mult)
+            nc.gpsimd.tensor_tensor(out=h_sb[:], in0=held["tanh_c", g, j][:], in1=rows_of("o", g, j), op=ALU.mult)
             nc.sync.dma_start(out=h_v[:, g * GROUP + j, :], in_=h_sb[:])
 
-        def per_tile(step, lag, stage):
+        def per_tile(step, lag, *stages):
             t = step - lag
             if 0 <= t < TILES:
-                stage(t // GROUP, t % GROUP)
+                for stage in stages:
+                    stage(t // GROUP, t % GROUP)
 
-        def per_pair(step, lag, stage):
-            t = step - lag
-            if 0 <= t < TILES and t % 2 == 0:
-                stage(t // GROUP, (t % GROUP) // 2)
-
-        def per_group(step, lag, stage):
+        def per_group(step, lag, *stages):
             t = step - lag
             if 0 <= t < TILES and t % GROUP == 0:
-                stage(t // GROUP)
+                for stage in stages:
+                    stage(t // GROUP)
 
-        for step in range(AT_LOAD, TILES + AT_OUT):
-            per_group(step, AT_LOAD, load)
-            per_group(step, AT_LOAD_O, load_o)
+        for step in range(TILES + AT_OUT):
+            for b in range(len(LOADS) - 1):
+                if max(LOADS[b] - LOAD_AHEAD, 0) == step:
+                    load(b)
+                    if b == 0:
+                        load_weights()
+                    if b == 2:
+                        load_vectors()
+            for b in range(TILES // LOAD):
+                if b * LOAD - LOAD_O_AHEAD + AT_OUT == step:
+                    load_o(b)
+            per_tile(step, AT_DEVIATION, mean)
             per_tile(step, AT_OUT, squash)
-            per_pair(step, AT_INV_STD, inv_std)
-            per_group(step, AT_ALPHA, root_h)
-            per_group(step, AT_ROOT_MAIN, root_main)
-            per_tile(step, AT_OUT, gate_out)
-            per_tile(step, AT_CLIP, kept_main)
-            per_tile(step, AT_PRODUCT, product)
-            per_tile(step, AT_CLIP, clip)
-            per_tile(step, AT_TURN, transpose_in)
-            per_tile(step, AT_MATMUL, gate_matmuls)
-            per_tile(step, AT_NORM_H, transpose_back)
-            per_tile(step, AT_CLIP - 1, transpose_back)
-            per_tile(step, AT_BLEND, blend)
             per_tile(step, AT_NORM_MAIN, norm_main)
-            per_tile(step, AT_TURN, copy_in)
-            per_tile(step, AT_MATMUL, relu_gate)
-            per_tile(step, AT_DEVIATION, deviation)
-            per_tile(step, AT_NORM_H, norm_h)
-            per_pair(step, AT_VARIANCE, variance)
+            per_tile(step, AT_TURN, transpose_in)
+            if step == 0:
+                prepare_biases()
+                prepare_bag()
+            if step == GROUP + 1:
+                prepare_vectors()
+            per_tile(step, AT_PRODUCT, product)
+            per_group(step, AT_VARIANCE, variance)
+            per_group(step, AT_ALPHA, roots)
+            per_tile(step, AT_NORM_H, transpose_back)
+            per_tile(step, AT_CENTRE, centre)
+            per_tile(step, AT_OUT, gate_out)
             per_group(step, AT_ALPHA, clip_factor)
+            per_group(step, AT_VARIANCE, inv_std)
+            per_tile(step, AT_TURN, copy_in)
+            per_tile(step, AT_BLEND, blend)
+            per_tile(step, AT_NORM_H, norm_h)
+            per_tile(step, AT_CLIP, transpose_back, clip)
+            per_tile(step, AT_MATMUL, gate_matmuls)
+            per_tile(step, AT_DEVIATION, deviation)
             per_group(step, AT_QUANTISE, quantise)
+            per_tile(step, AT_MATMUL, relu_gate)
+            per_tile(step, AT_EMB, emb)
+            per_tile(step, AT_TURN, kept_main)

@@ -29,6 +29,7 @@ BAG_EPS = 1e-6
 FLOPS = 2 * B * (2 * H + H) * H
 
 AT_TURN = 0
+AT_KEPT_MAIN = 1
 AT_QUANTISE = AT_TURN + GROUP - 1
 AT_NORM_MAIN = 2
 AT_MATMUL = AT_QUANTISE + 1
@@ -252,14 +253,28 @@ def tile_bag_lstm_pb_t_kernel(
             nc.gpsimd.tensor_tensor(out=norms[:], in0=held["norm_sq", g][:], in1=half[:], op=ALU.pow)
             held["norms", g] = norms
 
-        def clip_factor(g):
-            em, hm = held["norms", g][:, 0, :], held["norms", g][:, 1, :]
+        def clip_denominator(g):
             denom = small.tile([P, GROUP], F32)
-            nc.vector.scalar_tensor_tensor(out=denom[:], in0=hm, scalar=BAG_EPS, in1=em, op0=ALU.add, op1=ALU.max)
+            em, hm = held["norms", g][:, 0, :], held["norms", g][:, 1, :]
+            for j in range(GROUP):
+                nc.vector.tensor_scalar(
+                    out=denom[:, j : j + 1], in0=hm[:, j : j + 1], scalar1=BAG_EPS, scalar2=em[:, j : j + 1],
+                    op0=ALU.add, op1=ALU.max,
+                )
+            held["denom", g] = denom
+
+        def clip_reciprocal(g):
             recip = small.tile([P, GROUP], F32)
-            nc.vector.reciprocal(out=recip[:], in_=denom[:])
+            nc.vector.reciprocal(out=recip[:], in_=held["denom", g][:])
+            held["recip", g] = recip
+
+        def clip_factor(g):
             alpha = small.tile([P, GROUP], F32)
-            nc.vector.tensor_mul(out=alpha[:], in0=recip[:], in1=em)
+            em = held["norms", g][:, 0, :]
+            for j in range(GROUP):
+                nc.vector.tensor_scalar_mul(
+                    out=alpha[:, j : j + 1], in0=held["recip", g][:, j : j + 1], scalar1=em[:, j : j + 1]
+                )
             held["alpha", g] = alpha
 
         def clip(g, j):
@@ -295,7 +310,7 @@ def tile_bag_lstm_pb_t_kernel(
 
         def variance(g):
             var_eps = small.tile([P, GROUP], F32)
-            nc.vector.tensor_scalar(
+            nc.gpsimd.tensor_scalar(
                 out=var_eps[:], in0=held["dev_sq", g][:], scalar1=1.0 / H, scalar2=LN_EPS, op0=ALU.mult, op1=ALU.add
             )
             held["var_eps", g] = var_eps
@@ -366,15 +381,17 @@ def tile_bag_lstm_pb_t_kernel(
             if step == GROUP + 1:
                 prepare_vectors()
             per_tile(step, AT_PRODUCT, product)
-            per_group(step, AT_VARIANCE, variance)
             per_group(step, AT_ALPHA, roots)
             per_tile(step, AT_NORM_H, transpose_back)
+            per_group(step, AT_ALPHA, clip_denominator)
             per_tile(step, AT_CENTRE, centre)
+            per_group(step, AT_ALPHA, clip_reciprocal)
+            per_tile(step, AT_KEPT_MAIN, kept_main)
             per_tile(step, AT_OUT, gate_out)
-            per_group(step, AT_ALPHA, clip_factor)
-            per_group(step, AT_VARIANCE, inv_std)
+            per_group(step, AT_VARIANCE, variance, inv_std)
             per_tile(step, AT_TURN, copy_in)
             per_tile(step, AT_BLEND, blend)
+            per_group(step, AT_ALPHA, clip_factor)
             per_tile(step, AT_NORM_H, norm_h)
             per_tile(step, AT_CLIP, transpose_back, clip)
             per_tile(step, AT_MATMUL, gate_matmuls)
@@ -382,4 +399,3 @@ def tile_bag_lstm_pb_t_kernel(
             per_group(step, AT_QUANTISE, quantise)
             per_tile(step, AT_MATMUL, relu_gate)
             per_tile(step, AT_EMB, emb)
-            per_tile(step, AT_TURN, kept_main)

@@ -112,7 +112,7 @@ def tile_bag_lstm_pb_t_kernel(
 
         def prepare_biases():
             nc.vector.tensor_copy(out=bias_rows_f[:], in_=bias_rows[:])
-            bias_ps = psum.tile([P, P], F32, tag="turned", bufs=3)
+            bias_ps = psum.tile([P, P], F32, tag="turned", bufs=2)
             nc.tensor.transpose(bias_ps[:], bias_rows_f[:], ident[:])
             nc.vector.tensor_copy(out=bias_cols[:], in_=bias_ps[:, 0 : 2 * CHUNKS])
 
@@ -145,7 +145,7 @@ def tile_bag_lstm_pb_t_kernel(
             return held[name, g * GROUP + j]
 
         def transpose_in(g, j):
-            xt = psum.tile([P, 2, 2, P], F32, tag="turned", bufs=3)
+            xt = psum.tile([P, 2, 2, P], F32, tag="turned", bufs=2)
             for x, name in enumerate(("main", "branch")):
                 words = rows_of(name, g, j).bitcast(F32)
                 for u in range(2):
@@ -183,8 +183,8 @@ def tile_bag_lstm_pb_t_kernel(
             )
 
         def gate_matmuls(g, s):
-            gate_ps = psum.tile([P, SHARE, ROWS], F32, tag="gate")
-            value_ps = psum.tile([P, SHARE, ROWS], F32, tag="value")
+            gate_ps = psum.tile([P, SHARE, ROWS], F32, tag="gate", bufs=1)
+            value_ps = psum.tile([P, SHARE, ROWS], F32, tag="value", bufs=1)
             for i in range(SHARE):
                 for j in range(GROUP):
                     rows = slice(j * P, (j + 1) * P)
@@ -237,7 +237,7 @@ def tile_bag_lstm_pb_t_kernel(
             held["wm", g, j] = wm
 
         def transpose_back(g, j):
-            h_ps = psum.tile([P, H], F32, tag="turned", bufs=3)
+            h_ps = psum.tile([P, H], F32, tag="h", bufs=3)
             for c in range(CHUNKS):
                 nc.tensor.transpose(h_ps[:, c * P : (c + 1) * P], held["hT", g][:, c, j * P : (j + 1) * P], ident[:])
             held["h", g, j] = h_ps
@@ -393,7 +393,7 @@ def tile_bag_lstm_pb_t_kernel(
             per_tile(step, AT_BLEND, blend)
             per_group(step, AT_ALPHA, clip_factor)
             per_tile(step, AT_NORM_H, norm_h)
-            per_tile(step, AT_CLIP, transpose_back, clip)
+            per_tile(step, AT_CLIP, clip)
             per_tile(step, AT_MATMUL, gate_matmuls)
             per_tile(step, AT_DEVIATION, deviation)
             per_group(step, AT_QUANTISE, quantise)

@@ -30,16 +30,16 @@ FLOPS = 2 * B * (2 * H + H) * H
 
 AT_TURN = 0
 AT_KEPT_MAIN = 1
-AT_QUANTISE = AT_TURN + GROUP - 1
 AT_NORM_MAIN = 2
-AT_MATMUL = AT_QUANTISE + 1
+AT_QUANTISE = AT_TURN + GROUP - 1
+AT_MATMUL = AT_QUANTISE + 2
 AT_PRODUCT = AT_MATMUL + 1
-AT_NORM_H = AT_PRODUCT + GROUP - 1
+AT_NORM_H = AT_PRODUCT + GROUP
 AT_ALPHA = AT_NORM_H + GROUP
 AT_CLIP = AT_ALPHA
 AT_DEVIATION = AT_CLIP + 1
-AT_CENTRE = AT_DEVIATION + 1
 AT_VARIANCE = AT_DEVIATION + GROUP
+AT_CENTRE = AT_VARIANCE
 AT_EMB = AT_VARIANCE
 AT_BLEND = AT_EMB + 1
 AT_OUT = AT_BLEND + 2
@@ -128,7 +128,7 @@ def tile_bag_lstm_pb_t_kernel(
 
         def load(b):
             first, end = LOADS[b], LOADS[b + 1]
-            main_sb = inputs.tile([P, LOAD, H], BF16, tag="main", bufs=6)
+            main_sb = inputs.tile([P, LOAD, H], BF16, tag="main", bufs=7)
             nc.sync.dma_start(out=main_sb[:, 0 : end - first, :], in_=main_v[:, first:end, :])
             branch_sb = inputs.tile([P, LOAD, H], BF16, tag="branch", bufs=4)
             nc.sync.dma_start(out=branch_sb[:, 0 : end - first, :], in_=branch_v[:, first:end, :])
@@ -371,31 +371,30 @@ def tile_bag_lstm_pb_t_kernel(
             for b in range(TILES // LOAD):
                 if b * LOAD - LOAD_O_AHEAD + AT_OUT == step:
                     load_o(b)
-            per_tile(step, AT_DEVIATION, mean)
-            per_tile(step, AT_OUT, squash)
-            per_tile(step, AT_NORM_MAIN, norm_main)
             per_tile(step, AT_TURN, transpose_in)
             if step == 0:
                 prepare_biases()
                 prepare_bag()
             if step == GROUP + 1:
                 prepare_vectors()
-            per_tile(step, AT_PRODUCT, product)
-            per_group(step, AT_ALPHA, roots)
-            per_tile(step, AT_NORM_H, transpose_back)
-            per_group(step, AT_ALPHA, clip_denominator)
+            per_group(step, AT_ALPHA, roots, clip_denominator)
+            per_tile(step, AT_DEVIATION, mean)
             per_tile(step, AT_CENTRE, centre)
-            per_group(step, AT_ALPHA, clip_reciprocal)
-            per_tile(step, AT_KEPT_MAIN, kept_main)
-            per_tile(step, AT_OUT, gate_out)
             per_group(step, AT_VARIANCE, variance, inv_std)
+            per_group(step, AT_ALPHA, clip_reciprocal)
+            per_tile(step, AT_OUT, squash)
+            per_tile(step, AT_KEPT_MAIN, kept_main)
+            per_tile(step, AT_NORM_MAIN, norm_main)
+            per_tile(step, AT_NORM_H, transpose_back)
             per_tile(step, AT_TURN, copy_in)
-            per_tile(step, AT_BLEND, blend)
-            per_group(step, AT_ALPHA, clip_factor)
             per_tile(step, AT_NORM_H, norm_h)
-            per_tile(step, AT_CLIP, clip)
             per_tile(step, AT_MATMUL, gate_matmuls)
-            per_tile(step, AT_DEVIATION, deviation)
+            per_tile(step, AT_PRODUCT, product)
+            per_group(step, AT_ALPHA, clip_factor)
+            per_tile(step, AT_OUT, gate_out)
+            per_tile(step, AT_BLEND, blend)
+            per_tile(step, AT_CLIP, clip)
             per_group(step, AT_QUANTISE, quantise)
-            per_tile(step, AT_MATMUL, relu_gate)
+            per_tile(step, AT_DEVIATION, deviation)
             per_tile(step, AT_EMB, emb)
+            per_tile(step, AT_MATMUL, relu_gate)

@@ -29,19 +29,18 @@ BAG_EPS = 1e-6
 FLOPS = 2 * B * (2 * H + H) * H
 
 AT_TURN = 0
-AT_KEPT_MAIN = 1
-AT_NORM_MAIN = 2
 AT_QUANTISE = AT_TURN + GROUP - 1
-AT_MATMUL = AT_QUANTISE + 2
+AT_NORM_MAIN = 1
+AT_MATMUL = AT_QUANTISE + 1
 AT_PRODUCT = AT_MATMUL + 1
 AT_NORM_H = AT_PRODUCT + GROUP
+AT_KEPT = 6
 AT_ALPHA = AT_NORM_H + GROUP
 AT_CLIP = AT_ALPHA
 AT_DEVIATION = AT_CLIP + 1
+AT_CENTRE = AT_DEVIATION
 AT_VARIANCE = AT_DEVIATION + GROUP
-AT_CENTRE = AT_VARIANCE
-AT_EMB = AT_VARIANCE
-AT_BLEND = AT_EMB + 1
+AT_BLEND = AT_VARIANCE
 AT_OUT = AT_BLEND + 2
 LOAD_AHEAD = 6
 LOAD_O_AHEAD = 5
@@ -84,9 +83,9 @@ def tile_bag_lstm_pb_t_kernel(
         minus_half = consts.tile([P, GROUP], F32)
         nc.gpsimd.memset(minus_half[:], -0.5)
         bias_cols = consts.tile([P, 2 * CHUNKS], F32)
-        ln_ps = psum.tile([P, 2, H], BF16, tag="ln", bufs=1)
-        gain = ln_ps[:, 0, :]
-        shift = ln_ps[:, 1, :]
+        gain = psum.tile([P, H], BF16, tag="gain", bufs=1)
+        bag_row = consts.tile([P, P, TILES], BF16)
+        nc.vector.memset(bag_row[:], 0.0)
         bag = consts.tile([P, TILES], F32)
         one_minus_bag = consts.tile([P, TILES], F32)
         bias_rows_f = consts.tile([P, P], F32)
@@ -102,17 +101,19 @@ def tile_bag_lstm_pb_t_kernel(
                     in_=W_mb_scales[:, q_rows, :].rearrange("g q n -> q g n").bitcast(I32),
                 )
                 nc.sync.dma_start(out=w_scales[live_rows, 2, :].bitcast(I32), in_=W_b_scales[0, q_rows, :].bitcast(I32))
-            nc.sync.dma_start(out=bias_rows[0:CHUNKS, :], in_=b_mb.rearrange("(c p) -> c p", p=P))
-            nc.sync.dma_start(out=bias_rows[CHUNKS : 2 * CHUNKS, :], in_=b_b.rearrange("(c p) -> c p", p=P))
-            nc.sync.dma_start(out=bag_bf[:], in_=is_bag.rearrange("(p t) o -> p (t o)", t=TILES))
 
-        def load_vectors():
-            nc.sync.dma_start(out=ln_rows[0:1, 0, :], in_=ln_g.rearrange("(o f) -> o f", o=1))
-            nc.sync.dma_start(out=ln_rows[0:1, 1, :], in_=ln_b.rearrange("(o f) -> o f", o=1))
+        nc.gpsimd.dma_start(out=bias_rows[0:CHUNKS, :], in_=b_mb.rearrange("(c p) -> c p", p=P))
+        nc.gpsimd.dma_start(out=bias_rows[CHUNKS : 2 * CHUNKS, :], in_=b_b.rearrange("(c p) -> c p", p=P))
+        nc.gpsimd.dma_start(out=bag_bf[:], in_=is_bag.rearrange("(p t) o -> p (t o)", t=TILES))
+        nc.gpsimd.dma_start(
+            out=bag_row[0:1, :, :].rearrange("k p t -> k (p t)"), in_=is_bag.rearrange("b o -> o b")
+        )
+        nc.gpsimd.dma_start(out=ln_rows[0:1, 0, :], in_=ln_g.rearrange("(o f) -> o f", o=1))
+        nc.gpsimd.dma_start(out=ln_rows[0:1, 1, :], in_=ln_b.rearrange("(o f) -> o f", o=1))
 
         def prepare_biases():
             nc.vector.tensor_copy(out=bias_rows_f[:], in_=bias_rows[:])
-            bias_ps = psum.tile([P, P], F32, tag="turned", bufs=2)
+            bias_ps = psum.tile([P, P], F32, tag="turned", bufs=1)
             nc.tensor.transpose(bias_ps[:], bias_rows_f[:], ident[:])
             nc.vector.tensor_copy(out=bias_cols[:], in_=bias_ps[:, 0 : 2 * CHUNKS])
 
@@ -122,9 +123,8 @@ def tile_bag_lstm_pb_t_kernel(
                 out=one_minus_bag[:], in0=bag[:], scalar1=-1.0, scalar2=1.0, op0=ALU.mult, op1=ALU.add
             )
 
-        def prepare_vectors():
-            nc.tensor.matmul(out=gain, lhsT=ones[:], rhs=ln_rows[:, 0, :], start=True, stop=True)
-            nc.tensor.matmul(out=shift, lhsT=ones[:], rhs=ln_rows[:, 1, :], start=True, stop=True)
+        def prepare_gain():
+            nc.tensor.matmul(out=gain[:], lhsT=ones[:], rhs=ln_rows[:, 0, :], start=True, stop=True)
 
         def load(b):
             first, end = LOADS[b], LOADS[b + 1]
@@ -145,7 +145,7 @@ def tile_bag_lstm_pb_t_kernel(
             return held[name, g * GROUP + j]
 
         def transpose_in(g, j):
-            xt = psum.tile([P, 2, 2, P], F32, tag="turned", bufs=2)
+            xt = psum.tile([P, 2, 2, P], F32, tag="turned", bufs=1)
             for x, name in enumerate(("main", "branch")):
                 words = rows_of(name, g, j).bitcast(F32)
                 for u in range(2):
@@ -227,11 +227,18 @@ def tile_bag_lstm_pb_t_kernel(
                 out=unread_m[:], in_=rows_of("main", g, j), func=ACT.Square, accum_out=held["norm_sq", g][:, 0, j : j + 1]
             )
 
-        def kept_main(g, j):
+        def bag_shift(g, j):
+            shift_ps = psum.tile([P, H], F32, tag="shift", bufs=1)
+            nc.tensor.matmul(
+                out=shift_ps[:], lhsT=bag_row[:, :, g * GROUP + j], rhs=ln_rows[:, 1, :], start=True, stop=True
+            )
+            held["shift", g, j] = shift_ps
+
+        def kept(g, j):
             t = g * GROUP + j
-            wm = work.tile([P, H], F32, bufs=12)
-            nc.gpsimd.tensor_scalar(
-                out=wm[:], in0=rows_of("main", g, j), scalar1=one_minus_bag[:, t : t + 1], scalar2=0.0,
+            wm = work.tile([P, H], F32, bufs=8)
+            nc.vector.scalar_tensor_tensor(
+                out=wm[:], in0=rows_of("main", g, j), scalar=one_minus_bag[:, t : t + 1], in1=held["shift", g, j][:],
                 op0=ALU.mult, op1=ALU.add,
             )
             held["wm", g, j] = wm
@@ -294,7 +301,7 @@ def tile_bag_lstm_pb_t_kernel(
         def centre(g, j):
             centred = work.tile([P, H], F32, bufs=3)
             nc.vector.scalar_tensor_tensor(
-                out=centred[:], in0=held["pre", g, j][:], scalar=held["negmu", g, j][:], in1=gain, op0=ALU.add, op1=ALU.mult
+                out=centred[:], in0=held["pre", g, j][:], scalar=held["negmu", g, j][:], in1=gain[:], op0=ALU.add, op1=ALU.mult
             )
             held["centred", g, j] = centred
 
@@ -318,21 +325,15 @@ def tile_bag_lstm_pb_t_kernel(
         def inv_std(g):
             rstd = small.tile([P, GROUP], F32)
             nc.gpsimd.tensor_tensor(out=rstd[:], in0=held["var_eps", g][:], in1=minus_half[:], op=ALU.pow)
-            held["rstd", g] = rstd
-
-        def emb(g, j):
-            emb = work.tile([P, H], F32, bufs=3)
-            nc.vector.scalar_tensor_tensor(
-                out=emb[:], in0=held["centred", g, j][:], scalar=held["rstd", g][:, j : j + 1], in1=shift,
-                op0=ALU.mult, op1=ALU.add,
-            )
-            held["emb", g, j] = emb
+            factor = small.tile([P, GROUP], F32)
+            nc.gpsimd.tensor_mul(out=factor[:], in0=rstd[:], in1=bag[:, g * GROUP : (g + 1) * GROUP])
+            held["factor", g] = factor
 
         def blend(g, j):
             t = g * GROUP + j
             shift_c = work.tile([P, H], F32, bufs=5)
             nc.vector.scalar_tensor_tensor(
-                out=shift_c[:], in0=held["emb", g, j][:], scalar=bag[:, t : t + 1], in1=held["wm", g, j][:],
+                out=shift_c[:], in0=held["centred", g, j][:], scalar=held["factor", g][:, j : j + 1], in1=held["wm", g, j][:],
                 op0=ALU.mult, op1=ALU.add,
             )
             nc.sync.dma_start(out=shift_v[:, t, :], in_=shift_c[:])
@@ -364,37 +365,36 @@ def tile_bag_lstm_pb_t_kernel(
             for b in range(len(LOADS) - 1):
                 if max(LOADS[b] - LOAD_AHEAD, 0) == step:
                     load(b)
-                    if b == 0:
-                        load_weights()
                     if b == 2:
-                        load_vectors()
+                        load_weights()
             for b in range(TILES // LOAD):
                 if b * LOAD - LOAD_O_AHEAD + AT_OUT == step:
                     load_o(b)
+            per_group(step, AT_ALPHA, roots)
+            per_tile(step, AT_PRODUCT, product)
             per_tile(step, AT_TURN, transpose_in)
-            if step == 0:
+            if step == GROUP:
                 prepare_biases()
                 prepare_bag()
-            if step == GROUP + 1:
-                prepare_vectors()
-            per_group(step, AT_ALPHA, roots, clip_denominator)
-            per_tile(step, AT_DEVIATION, mean)
-            per_tile(step, AT_CENTRE, centre)
+            if step == AT_CLIP:
+                prepare_gain()
             per_group(step, AT_VARIANCE, variance, inv_std)
-            per_group(step, AT_ALPHA, clip_reciprocal)
             per_tile(step, AT_OUT, squash)
-            per_tile(step, AT_KEPT_MAIN, kept_main)
-            per_tile(step, AT_NORM_MAIN, norm_main)
-            per_tile(step, AT_NORM_H, transpose_back)
-            per_tile(step, AT_TURN, copy_in)
-            per_tile(step, AT_NORM_H, norm_h)
-            per_tile(step, AT_MATMUL, gate_matmuls)
-            per_tile(step, AT_PRODUCT, product)
-            per_group(step, AT_ALPHA, clip_factor)
+            per_tile(step, AT_DEVIATION, mean)
             per_tile(step, AT_OUT, gate_out)
-            per_tile(step, AT_BLEND, blend)
-            per_tile(step, AT_CLIP, clip)
-            per_group(step, AT_QUANTISE, quantise)
+            per_group(step, AT_ALPHA, clip_denominator)
+            per_tile(step, AT_KEPT, kept)
+            per_tile(step, AT_NORM_MAIN, norm_main)
+            per_group(step, AT_ALPHA, clip_reciprocal)
+            per_tile(step, AT_TURN, copy_in)
+            per_tile(step, AT_NORM_H, transpose_back)
+            per_tile(step, AT_MATMUL, gate_matmuls)
+            per_tile(step, AT_KEPT - 1, bag_shift)
+            per_tile(step, AT_NORM_H, norm_h)
+            per_group(step, AT_ALPHA, clip_factor)
             per_tile(step, AT_DEVIATION, deviation)
-            per_tile(step, AT_EMB, emb)
+            per_group(step, AT_QUANTISE, quantise)
+            per_tile(step, AT_CLIP, clip)
+            per_tile(step, AT_BLEND, blend)
+            per_tile(step, AT_CENTRE, centre)
             per_tile(step, AT_MATMUL, relu_gate)

@@ -34,7 +34,7 @@ AT_NORM_MAIN = 1
 AT_MATMUL = AT_QUANTISE + 1
 AT_PRODUCT = AT_MATMUL + 1
 AT_NORM_H = AT_PRODUCT + GROUP
-AT_KEPT = 6
+AT_KEPT = 8
 AT_ALPHA = AT_NORM_H + GROUP
 AT_CLIP = AT_ALPHA
 AT_DEVIATION = AT_CLIP + 1
@@ -85,14 +85,15 @@ def tile_bag_lstm_pb_t_kernel(
         bias_cols = consts.tile([P, 2 * CHUNKS], F32)
         gain = psum.tile([P, H], BF16, tag="gain", bufs=1)
         bag_row = consts.tile([P, P, TILES], BF16)
-        nc.vector.memset(bag_row[:], 0.0)
         bag = consts.tile([P, TILES], F32)
         one_minus_bag = consts.tile([P, TILES], F32)
         bias_rows_f = consts.tile([P, P], F32)
 
-        def load_weights():
+        def load_words():
             nc.sync.dma_start(out=w_words[:, 0:2, :].bitcast(I32), in_=W_mb_words.rearrange("g p b -> p g b").bitcast(I32))
             nc.sync.dma_start(out=w_words[:, 2, :].bitcast(I32), in_=W_b_words[0].bitcast(I32))
+
+        def load_scales():
             for quad in range(4):
                 live_rows = slice(32 * quad, 32 * quad + 4)
                 q_rows = slice(4 * quad, 4 * quad + 4)
@@ -105,15 +106,16 @@ def tile_bag_lstm_pb_t_kernel(
         nc.gpsimd.dma_start(out=bias_rows[0:CHUNKS, :], in_=b_mb.rearrange("(c p) -> c p", p=P))
         nc.gpsimd.dma_start(out=bias_rows[CHUNKS : 2 * CHUNKS, :], in_=b_b.rearrange("(c p) -> c p", p=P))
         nc.gpsimd.dma_start(out=bag_bf[:], in_=is_bag.rearrange("(p t) o -> p (t o)", t=TILES))
+        nc.gpsimd.dma_start(out=ln_rows[0:1, 0, :], in_=ln_g.rearrange("(o f) -> o f", o=1))
+        nc.gpsimd.dma_start(out=ln_rows[0:1, 1, :], in_=ln_b.rearrange("(o f) -> o f", o=1))
+        nc.gpsimd.memset(bag_row[:].rearrange("k p t -> k (p t)").bitcast(I32), 0)
         nc.gpsimd.dma_start(
             out=bag_row[0:1, :, :].rearrange("k p t -> k (p t)"), in_=is_bag.rearrange("b o -> o b")
         )
-        nc.gpsimd.dma_start(out=ln_rows[0:1, 0, :], in_=ln_g.rearrange("(o f) -> o f", o=1))
-        nc.gpsimd.dma_start(out=ln_rows[0:1, 1, :], in_=ln_b.rearrange("(o f) -> o f", o=1))
 
         def prepare_biases():
             nc.vector.tensor_copy(out=bias_rows_f[:], in_=bias_rows[:])
-            bias_ps = psum.tile([P, P], F32, tag="turned", bufs=1)
+            bias_ps = psum.tile([P, P], F32, tag="shift", bufs=1)
             nc.tensor.transpose(bias_ps[:], bias_rows_f[:], ident[:])
             nc.vector.tensor_copy(out=bias_cols[:], in_=bias_ps[:, 0 : 2 * CHUNKS])
 
@@ -145,7 +147,10 @@ def tile_bag_lstm_pb_t_kernel(
             return held[name, g * GROUP + j]
 
         def transpose_in(g, j):
-            xt = psum.tile([P, 2, 2, P], F32, tag="turned", bufs=1)
+            if g * GROUP + j <= GROUP:
+                xt = psum.tile([P, 2, 2, P], F32, tag="h", bufs=3)
+            else:
+                xt = psum.tile([P, 2, 2, P], F32, tag="turned", bufs=1)
             for x, name in enumerate(("main", "branch")):
                 words = rows_of(name, g, j).bitcast(F32)
                 for u in range(2):
@@ -262,12 +267,9 @@ def tile_bag_lstm_pb_t_kernel(
 
         def clip_denominator(g):
             denom = small.tile([P, GROUP], F32)
-            em, hm = held["norms", g][:, 0, :], held["norms", g][:, 1, :]
-            for j in range(GROUP):
-                nc.vector.tensor_scalar(
-                    out=denom[:, j : j + 1], in0=hm[:, j : j + 1], scalar1=BAG_EPS, scalar2=em[:, j : j + 1],
-                    op0=ALU.add, op1=ALU.max,
-                )
+            nc.gpsimd.tensor_scalar(
+                out=denom[:], in0=held["norms", g][:, 1, :], scalar1=1.0, scalar2=BAG_EPS, op0=ALU.mult, op1=ALU.add
+            )
             held["denom", g] = denom
 
         def clip_reciprocal(g):
@@ -277,10 +279,10 @@ def tile_bag_lstm_pb_t_kernel(
 
         def clip_factor(g):
             alpha = small.tile([P, GROUP], F32)
-            em = held["norms", g][:, 0, :]
             for j in range(GROUP):
-                nc.vector.tensor_scalar_mul(
-                    out=alpha[:, j : j + 1], in0=held["recip", g][:, j : j + 1], scalar1=em[:, j : j + 1]
+                nc.vector.tensor_scalar(
+                    out=alpha[:, j : j + 1], in0=held["recip", g][:, j : j + 1], scalar1=held["norms", g][:, 0, j : j + 1],
+                    scalar2=1.0, op0=ALU.mult, op1=ALU.min,
                 )
             held["alpha", g] = alpha
 
@@ -365,16 +367,19 @@ def tile_bag_lstm_pb_t_kernel(
             for b in range(len(LOADS) - 1):
                 if max(LOADS[b] - LOAD_AHEAD, 0) == step:
                     load(b)
+                    if b == 1:
+                        load_words()
                     if b == 2:
-                        load_weights()
+                        load_scales()
             for b in range(TILES // LOAD):
                 if b * LOAD - LOAD_O_AHEAD + AT_OUT == step:
                     load_o(b)
-            per_group(step, AT_ALPHA, roots)
+            per_group(step, AT_ALPHA, roots, clip_denominator)
             per_tile(step, AT_PRODUCT, product)
             per_tile(step, AT_TURN, transpose_in)
             if step == GROUP:
                 prepare_biases()
+            if step == 2 * GROUP:
                 prepare_bag()
             if step == AT_CLIP:
                 prepare_gain()
@@ -382,7 +387,6 @@ def tile_bag_lstm_pb_t_kernel(
             per_tile(step, AT_OUT, squash)
             per_tile(step, AT_DEVIATION, mean)
             per_tile(step, AT_OUT, gate_out)
-            per_group(step, AT_ALPHA, clip_denominator)
             per_tile(step, AT_KEPT, kept)
             per_tile(step, AT_NORM_MAIN, norm_main)
             per_group(step, AT_ALPHA, clip_reciprocal)

@@ -30,18 +30,19 @@ FLOPS = 2 * B * (2 * H + H) * H
 
 AT_TURN = 0
 AT_QUANTISE = AT_TURN + GROUP - 1
-AT_NORM_MAIN = 1
+AT_NORM_MAIN = 2
 AT_MATMUL = AT_QUANTISE + 1
 AT_PRODUCT = AT_MATMUL + 1
 AT_NORM_H = AT_PRODUCT + GROUP
-AT_KEPT = 8
+AT_KEPT = 7
 AT_ALPHA = AT_NORM_H + GROUP
 AT_CLIP = AT_ALPHA
 AT_DEVIATION = AT_CLIP + 1
-AT_CENTRE = AT_DEVIATION
 AT_VARIANCE = AT_DEVIATION + GROUP
+AT_CENTRE = AT_VARIANCE
 AT_BLEND = AT_VARIANCE
-AT_OUT = AT_BLEND + 2
+AT_SQUASH = AT_BLEND + 1
+AT_OUT = AT_SQUASH + 1
 LOAD_AHEAD = 6
 LOAD_O_AHEAD = 5
 
@@ -76,6 +77,8 @@ def tile_bag_lstm_pb_t_kernel(
         nc.vector.memset(ln_rows[:], 0.0)
         ones = consts.tile([P, P], BF16)
         nc.vector.memset(ones[:], 1.0)
+        bag_row = consts.tile([P, P, TILES], BF16)
+        nc.vector.memset(bag_row[:].rearrange("k p t -> k (p t)").bitcast(I32), 0)
         bag_bf = consts.tile([P, TILES], BF16)
         w_words = consts.tile([P, PASSES, 2 * H], U8, align_bytes=64)
         half = consts.tile([P, 2, GROUP], F32)
@@ -84,7 +87,6 @@ def tile_bag_lstm_pb_t_kernel(
         nc.gpsimd.memset(minus_half[:], -0.5)
         bias_cols = consts.tile([P, 2 * CHUNKS], F32)
         gain = psum.tile([P, H], BF16, tag="gain", bufs=1)
-        bag_row = consts.tile([P, P, TILES], BF16)
         bag = consts.tile([P, TILES], F32)
         one_minus_bag = consts.tile([P, TILES], F32)
         bias_rows_f = consts.tile([P, P], F32)
@@ -106,12 +108,11 @@ def tile_bag_lstm_pb_t_kernel(
         nc.gpsimd.dma_start(out=bias_rows[0:CHUNKS, :], in_=b_mb.rearrange("(c p) -> c p", p=P))
         nc.gpsimd.dma_start(out=bias_rows[CHUNKS : 2 * CHUNKS, :], in_=b_b.rearrange("(c p) -> c p", p=P))
         nc.gpsimd.dma_start(out=bag_bf[:], in_=is_bag.rearrange("(p t) o -> p (t o)", t=TILES))
-        nc.gpsimd.dma_start(out=ln_rows[0:1, 0, :], in_=ln_g.rearrange("(o f) -> o f", o=1))
-        nc.gpsimd.dma_start(out=ln_rows[0:1, 1, :], in_=ln_b.rearrange("(o f) -> o f", o=1))
-        nc.gpsimd.memset(bag_row[:].rearrange("k p t -> k (p t)").bitcast(I32), 0)
         nc.gpsimd.dma_start(
             out=bag_row[0:1, :, :].rearrange("k p t -> k (p t)"), in_=is_bag.rearrange("b o -> o b")
         )
+        nc.gpsimd.dma_start(out=ln_rows[0:1, 1, :], in_=ln_b.rearrange("(o f) -> o f", o=1))
+        nc.gpsimd.dma_start(out=ln_rows[0:1, 0, :], in_=ln_g.rearrange("(o f) -> o f", o=1))
 
         def prepare_biases():
             nc.vector.tensor_copy(out=bias_rows_f[:], in_=bias_rows[:])
@@ -208,11 +209,11 @@ def tile_bag_lstm_pb_t_kernel(
                 )
             held["weight_b", g, s] = weight_b
 
-        def product(g, s):
-            if s == 0:
-                hT = work.tile([P, CHUNKS, ROWS], F32, bufs=3)
-                held["hT", g] = hT
-            for i in range(SHARE):
+        def product(i):
+            def stage(g, s):
+                if s == 0 and i == 0:
+                    hT = work.tile([P, CHUNKS, ROWS], F32, bufs=3)
+                    held["hT", g] = hT
                 c = SHARE * s + i
                 nc.vector.scalar_tensor_tensor(
                     out=held["hT", g][:, c, :],
@@ -222,6 +223,8 @@ def tile_bag_lstm_pb_t_kernel(
                     op0=ALU.add,
                     op1=ALU.mult,
                 )
+
+            return stage
 
         def norm_main(g, j):
             if j == 0:
@@ -267,9 +270,12 @@ def tile_bag_lstm_pb_t_kernel(
 
         def clip_denominator(g):
             denom = small.tile([P, GROUP], F32)
-            nc.gpsimd.tensor_scalar(
-                out=denom[:], in0=held["norms", g][:, 1, :], scalar1=1.0, scalar2=BAG_EPS, op0=ALU.mult, op1=ALU.add
-            )
+            em, hm = held["norms", g][:, 0, :], held["norms", g][:, 1, :]
+            for j in range(GROUP):
+                nc.vector.tensor_scalar(
+                    out=denom[:, j : j + 1], in0=hm[:, j : j + 1], scalar1=BAG_EPS, scalar2=em[:, j : j + 1],
+                    op0=ALU.add, op1=ALU.max,
+                )
             held["denom", g] = denom
 
         def clip_reciprocal(g):
@@ -279,15 +285,15 @@ def tile_bag_lstm_pb_t_kernel(
 
         def clip_factor(g):
             alpha = small.tile([P, GROUP], F32)
+            em = held["norms", g][:, 0, :]
             for j in range(GROUP):
-                nc.vector.tensor_scalar(
-                    out=alpha[:, j : j + 1], in0=held["recip", g][:, j : j + 1], scalar1=held["norms", g][:, 0, j : j + 1],
-                    scalar2=1.0, op0=ALU.mult, op1=ALU.min,
+                nc.vector.tensor_scalar_mul(
+                    out=alpha[:, j : j + 1], in0=held["recip", g][:, j : j + 1], scalar1=em[:, j : j + 1]
                 )
             held["alpha", g] = alpha
 
         def clip(g, j):
-            pre = work.tile([P, H], F32, bufs=3)
+            pre = work.tile([P, H], F32, bufs=4)
             pre_sum = small.tile([P, 1], F32)
             nc.vector.scalar_tensor_tensor(
                 out=pre[:], in0=held["h", g, j][:], scalar=held["alpha", g][:, j : j + 1], in1=rows_of("main", g, j),
@@ -374,8 +380,8 @@ def tile_bag_lstm_pb_t_kernel(
             for b in range(TILES // LOAD):
                 if b * LOAD - LOAD_O_AHEAD + AT_OUT == step:
                     load_o(b)
-            per_group(step, AT_ALPHA, roots, clip_denominator)
-            per_tile(step, AT_PRODUCT, product)
+            per_group(step, AT_ALPHA, roots)
+            per_tile(step, AT_PRODUCT, product(0))
             per_tile(step, AT_TURN, transpose_in)
             if step == GROUP:
                 prepare_biases()
@@ -383,22 +389,23 @@ def tile_bag_lstm_pb_t_kernel(
                 prepare_bag()
             if step == AT_CLIP:
                 prepare_gain()
-            per_group(step, AT_VARIANCE, variance, inv_std)
-            per_tile(step, AT_OUT, squash)
-            per_tile(step, AT_DEVIATION, mean)
-            per_tile(step, AT_OUT, gate_out)
-            per_tile(step, AT_KEPT, kept)
-            per_tile(step, AT_NORM_MAIN, norm_main)
-            per_group(step, AT_ALPHA, clip_reciprocal)
-            per_tile(step, AT_TURN, copy_in)
             per_tile(step, AT_NORM_H, transpose_back)
-            per_tile(step, AT_MATMUL, gate_matmuls)
-            per_tile(step, AT_KEPT - 1, bag_shift)
+            per_tile(step, AT_NORM_MAIN, norm_main)
+            per_tile(step, AT_KEPT, kept)
+            per_group(step, AT_ALPHA, clip_denominator)
+            per_tile(step, AT_DEVIATION, mean)
+            per_tile(step, AT_PRODUCT, product(1))
+            per_group(step, AT_VARIANCE, variance, inv_std)
+            per_tile(step, AT_TURN, copy_in)
             per_tile(step, AT_NORM_H, norm_h)
-            per_group(step, AT_ALPHA, clip_factor)
             per_tile(step, AT_DEVIATION, deviation)
+            per_group(step, AT_ALPHA, clip_reciprocal)
+            per_tile(step, AT_MATMUL, gate_matmuls, relu_gate)
+            per_tile(step, AT_CENTRE, centre)
+            per_group(step, AT_ALPHA, clip_factor)
+            per_tile(step, AT_KEPT - 1, bag_shift)
+            per_tile(step, AT_SQUASH, squash)
+            per_tile(step, AT_OUT, gate_out)
             per_group(step, AT_QUANTISE, quantise)
             per_tile(step, AT_CLIP, clip)
             per_tile(step, AT_BLEND, blend)
-            per_tile(step, AT_CENTRE, centre)
-            per_tile(step, AT_MATMUL, relu_gate)

@@ -22,6 +22,7 @@ CHUNKS = H // P
 SHARE = CHUNKS // GROUP
 LOAD = 4
 LOADS = [0, 1, 2] + list(range(4, TILES + 1, LOAD))
+LAST = 4
 PASSES = 3
 LN_EPS = 1e-5
 BAG_EPS = 1e-6
@@ -354,7 +355,8 @@ def tile_bag_lstm_pb_t_kernel(
 
         def gate_out(g, j):
             h_sb = work.tile([P, H], F32, bufs=3)
-            nc.gpsimd.tensor_tensor(out=h_sb[:], in0=held["tanh_c", g, j][:], in1=rows_of("o", g, j), op=ALU.mult)
+            engine = nc.gpsimd if g * GROUP + j < TILES - LAST else nc.vector
+            engine.tensor_tensor(out=h_sb[:], in0=held["tanh_c", g, j][:], in1=rows_of("o", g, j), op=ALU.mult)
             nc.sync.dma_start(out=h_v[:, g * GROUP + j, :], in_=h_sb[:])
 
         def per_tile(step, lag, *stages):

from contextlib import ExitStack

import concourse.mybir as mybir
from concourse.masks import make_identity

F32 = mybir.dt.float32
BF16 = mybir.dt.bfloat16
I32 = mybir.dt.int32
U8 = mybir.dt.uint8
U32 = mybir.dt.uint32
FP8X4 = mybir.dt.float8_e4m3fn_x4
FP4X4 = mybir.dt.float4_e2m1fn_x4
ALU = mybir.AluOpType
ACT = mybir.ActivationFunctionType

P = 128
B, H = 4096, 512
TILES = B // P
GROUP = 2
ROWS = GROUP * P
CHUNKS = H // P
SHARE = CHUNKS // GROUP
LOAD = 4
LOADS = [0, 1, 2] + list(range(4, TILES + 1, LOAD))
LAST = 4
PASSES = 3
LN_EPS = 1e-5
BAG_EPS = 1e-6

FLOPS = 2 * B * (2 * H + H) * H

AT_TURN = 0
AT_QUANTISE = AT_TURN + GROUP - 1
AT_NORM_MAIN = 2
AT_MATMUL = AT_QUANTISE + 1
AT_PRODUCT = AT_MATMUL + 1
AT_NORM_H = AT_PRODUCT + GROUP
AT_KEPT = 7
AT_ALPHA = AT_NORM_H + GROUP
AT_CLIP = AT_ALPHA
AT_DEVIATION = AT_CLIP + 1
AT_VARIANCE = AT_DEVIATION + GROUP
AT_CENTRE = AT_VARIANCE
AT_BLEND = AT_VARIANCE
AT_SQUASH = AT_BLEND + 1
AT_OUT = AT_SQUASH + 1
LOAD_AHEAD = 6
LOAD_O_AHEAD = 5


def tile_bag_lstm_pb_t_kernel(
    tc, main, branch, o, is_bag, W_mb_words, W_mb_scales, b_mb, W_b_words, W_b_scales, b_b, ln_g, ln_b, out_0, out_1
):
    nc = tc.nc
    main_v = main.rearrange("(p t) f -> p t f", t=TILES)
    branch_v = branch.rearrange("(p t) f -> p t f", t=TILES)
    o_v = o.rearrange("(p t) f -> p t f", t=TILES)
    h_v = out_0.rearrange("(p t) f -> p t f", t=TILES)
    shift_v = out_1.rearrange("(p t) f -> p t f", t=TILES)

    with ExitStack() as ctx:
        consts = ctx.enter_context(tc.tile_pool(name="consts", bufs=1))
        inputs = ctx.enter_context(tc.tile_pool(name="inputs", bufs=3))
        work = ctx.enter_context(tc.tile_pool(name="work", bufs=2))
        small = ctx.enter_context(tc.tile_pool(name="small", bufs=4))
        psum = ctx.enter_context(tc.psum_pool(name="psum", bufs=2))
        ctx.enter_context(tc.manual_schedule())

        held = {}

        ident = consts.tile([P, P], F32)
        make_identity(nc, ident[:])
        w_scales = consts.tile([P, PASSES, H], U8, align_bytes=64)
        nc.vector.memset(w_scales[:].bitcast(I32), 0)
        bias_rows = consts.tile([P, P], BF16)
        nc.vector.memset(bias_rows[:], 0.0)
        ln_rows = consts.tile([P, 2, H], BF16)
        nc.vector.memset(ln_rows[:], 0.0)
        ones = consts.tile([P, P], BF16)
        nc.vector.memset(ones[:], 1.0)
        bag_row = consts.tile([P, P, TILES], BF16)
        nc.vector.memset(bag_row[:].rearrange("k p t -> k (p t)").bitcast(I32), 0)
        bag_bf = consts.tile([P, TILES], BF16)
        w_words = consts.tile([P, PASSES, 2 * H], U8, align_bytes=64)
        half = consts.tile([P, 2, GROUP], F32)
        nc.gpsimd.memset(half[:], 0.5)
        minus_half = consts.tile([P, GROUP], F32)
        nc.gpsimd.memset(minus_half[:], -0.5)
        bias_cols = consts.tile([P, 2 * CHUNKS], F32)
        gain = psum.tile([P, H], BF16, tag="gain", bufs=1)
        bag = consts.tile([P, TILES], F32)
        one_minus_bag = consts.tile([P, TILES], F32)
        bias_rows_f = consts.tile([P, P], F32)

        def load_words():
            nc.sync.dma_start(out=w_words[:, 0:2, :].bitcast(I32), in_=W_mb_words.rearrange("g p b -> p g b").bitcast(I32))
            nc.sync.dma_start(out=w_words[:, 2, :].bitcast(I32), in_=W_b_words[0].bitcast(I32))

        def load_scales():
            for quad in range(4):
                live_rows = slice(32 * quad, 32 * quad + 4)
                q_rows = slice(4 * quad, 4 * quad + 4)
                nc.sync.dma_start(
                    out=w_scales[live_rows, 0:2, :].bitcast(I32),
                    in_=W_mb_scales[:, q_rows, :].rearrange("g q n -> q g n").bitcast(I32),
                )
                nc.sync.dma_start(out=w_scales[live_rows, 2, :].bitcast(I32), in_=W_b_scales[0, q_rows, :].bitcast(I32))

        nc.gpsimd.dma_start(out=bias_rows[0:CHUNKS, :], in_=b_mb.rearrange("(c p) -> c p", p=P))
        nc.gpsimd.dma_start(out=bias_rows[CHUNKS : 2 * CHUNKS, :], in_=b_b.rearrange("(c p) -> c p", p=P))
        nc.gpsimd.dma_start(out=bag_bf[:], in_=is_bag.rearrange("(p t) o -> p (t o)", t=TILES))
        nc.gpsimd.dma_start(
            out=bag_row[0:1, :, :].rearrange("k p t -> k (p t)"), in_=is_bag.rearrange("b o -> o b")
        )
        nc.gpsimd.dma_start(out=ln_rows[0:1, 1, :], in_=ln_b.rearrange("(o f) -> o f", o=1))
        nc.gpsimd.dma_start(out=ln_rows[0:1, 0, :], in_=ln_g.rearrange("(o f) -> o f", o=1))

        def prepare_biases():
            nc.vector.tensor_copy(out=bias_rows_f[:], in_=bias_rows[:])
            bias_ps = psum.tile([P, P], F32, tag="shift", bufs=1)
            nc.tensor.transpose(bias_ps[:], bias_rows_f[:], ident[:])
            nc.vector.tensor_copy(out=bias_cols[:], in_=bias_ps[:, 0 : 2 * CHUNKS])

        def prepare_bag():
            nc.vector.tensor_copy(out=bag[:], in_=bag_bf[:])
            nc.vector.tensor_scalar(
                out=one_minus_bag[:], in0=bag[:], scalar1=-1.0, scalar2=1.0, op0=ALU.mult, op1=ALU.add
            )

        def prepare_gain():
            nc.tensor.matmul(out=gain[:], lhsT=ones[:], rhs=ln_rows[:, 0, :], start=True, stop=True)

        def load(b):
            first, end = LOADS[b], LOADS[b + 1]
            main_sb = inputs.tile([P, LOAD, H], BF16, tag="main", bufs=7)
            nc.sync.dma_start(out=main_sb[:, 0 : end - first, :], in_=main_v[:, first:end, :])
            branch_sb = inputs.tile([P, LOAD, H], BF16, tag="branch", bufs=4)
            nc.sync.dma_start(out=branch_sb[:, 0 : end - first, :], in_=branch_v[:, first:end, :])
            for t in range(first, end):
                held["main", t], held["branch", t] = main_sb[:, t - first, :], branch_sb[:, t - first, :]

        def load_o(b):
            o_sb = inputs.tile([P, LOAD, H], BF16, tag="o", bufs=3)
            nc.sync.dma_start(out=o_sb[:], in_=o_v[:, b * LOAD : (b + 1) * LOAD, :])
            for i in range(LOAD):
                held["o", b * LOAD + i] = o_sb[:, i, :]

        def rows_of(name, g, j):
            return held[name, g * GROUP + j]

        def transpose_in(g, j):
            if g * GROUP + j <= GROUP:
                xt = psum.tile([P, 2, 2, P], F32, tag="h", bufs=3)
            else:
                xt = psum.tile([P, 2, 2, P], F32, tag="turned", bufs=1)
            for x, name in enumerate(("main", "branch")):
                words = rows_of(name, g, j).bitcast(F32)
                for u in range(2):
                    nc.tensor.transpose(xt[:, x, u, :], words[:, u : H // 2 : 2], ident[:])
            held["xt", g, j] = xt

        def copy_in(g, j):
            if j == 0:
                grouped = work.tile([P, 2, ROWS, 4], BF16, align_bytes=64)
                held["grouped", g] = grouped
            grouped_words = held["grouped", g][:].bitcast(F32)
            nc.scalar.copy(
                out=grouped_words[:, :, j * P : (j + 1) * P, :], in_=held["xt", g, j][:].rearrange("p x u r -> p x r u")
            )

        def quantise(g):
            codes = work.tile([P, 2, ROWS], U32, align_bytes=64)
            x_scales = work.tile([P, 2, ROWS], U8, align_bytes=64)
            nc.vector.quantize_mx(
                out=codes[:].rearrange("p x r -> p (x r)").bitcast(FP8X4),
                scales=x_scales[:].rearrange("p x r -> p (x r)"),
                in_=held["grouped", g][:].rearrange("p x r t -> p (x r t)"),
            )
            held["codes", g], held["x_scales", g] = codes, x_scales

        def mx_pass(acc, g, a, x, c, rows, start, stop):
            nc.tensor.matmul_mx(
                out=acc[:, rows],
                lhsT=w_words[:, a, 2 * P * c : 2 * P * (c + 1)].bitcast(FP4X4),
                lhsT_scale=w_scales[:, a, P * c : P * (c + 1)],
                rhs=held["codes", g][:, x, rows].bitcast(FP8X4),
                rhs_scale=held["x_scales", g][:, x, rows],
                start=start,
                stop=stop,
            )

        def gate_matmuls(g, s):
            gate_ps = psum.tile([P, SHARE, ROWS], F32, tag="gate", bufs=1)
            value_ps = psum.tile([P, SHARE, ROWS], F32, tag="value", bufs=1)
            for i in range(SHARE):
                for j in range(GROUP):
                    rows = slice(j * P, (j + 1) * P)
                    mx_pass(gate_ps[:, i, :], g, 0, 0, SHARE * s + i, rows, True, False)
                    mx_pass(gate_ps[:, i, :], g, 1, 1, SHARE * s + i, rows, False, True)
            for i in range(SHARE):
                mx_pass(value_ps[:, i, :], g, 2, 1, SHARE * s + i, slice(0, ROWS), True, True)
            held["gate", g, s], held["value", g, s] = gate_ps, value_ps

        def relu_gate(g, s):
            weight_b = work.tile([P, SHARE, ROWS], F32)
            for i in range(SHARE):
                c = SHARE * s + i
                nc.scalar.activation(
                    out=weight_b[:, i, :], in_=held["gate", g, s][:, i, :], func=ACT.Relu, bias=bias_cols[:, c : c + 1]
                )
            held["weight_b", g, s] = weight_b

        def product(i):
            def stage(g, s):
                if s == 0 and i == 0:
                    hT = work.tile([P, CHUNKS, ROWS], F32, bufs=3)
                    held["hT", g] = hT
                c = SHARE * s + i
                nc.vector.scalar_tensor_tensor(
                    out=held["hT", g][:, c, :],
                    in0=held["value", g, s][:, i, :],
                    scalar=bias_cols[:, CHUNKS + c : CHUNKS + c + 1],
                    in1=held["weight_b", g, s][:, i, :],
                    op0=ALU.add,
                    op1=ALU.mult,
                )

            return stage

        def norm_main(g, j):
            if j == 0:
                norm_sq = small.tile([P, 2, GROUP], F32)
                held["norm_sq", g] = norm_sq
            unread_m = work.tile([P, H], BF16, tag="unread", bufs=4)
            nc.scalar.activation(
                out=unread_m[:], in_=rows_of("main", g, j), func=ACT.Square, accum_out=held["norm_sq", g][:, 0, j : j + 1]
            )

        def bag_shift(g, j):
            shift_ps = psum.tile([P, H], F32, tag="shift", bufs=1)
            nc.tensor.matmul(
                out=shift_ps[:], lhsT=bag_row[:, :, g * GROUP + j], rhs=ln_rows[:, 1, :], start=True, stop=True
            )
            held["shift", g, j] = shift_ps

        def kept(g, j):
            t = g * GROUP + j
            wm = work.tile([P, H], F32, bufs=8)
            nc.vector.scalar_tensor_tensor(
                out=wm[:], in0=rows_of("main", g, j), scalar=one_minus_bag[:, t : t + 1], in1=held["shift", g, j][:],
                op0=ALU.mult, op1=ALU.add,
            )
            held["wm", g, j] = wm

        def transpose_back(g, j):
            h_ps = psum.tile([P, H], F32, tag="h", bufs=3)
            for c in range(CHUNKS):
                nc.tensor.transpose(h_ps[:, c * P : (c + 1) * P], held["hT", g][:, c, j * P : (j + 1) * P], ident[:])
            held["h", g, j] = h_ps

        def norm_h(g, j):
            unread_h = work.tile([P, H], BF16, tag="unread", bufs=4)
            nc.scalar.activation(
                out=unread_h[:], in_=held["h", g, j][:], func=ACT.Square, accum_out=held["norm_sq", g][:, 1, j : j + 1]
            )

        def roots(g):
            norms = small.tile([P, 2, GROUP], F32)
            nc.gpsimd.tensor_tensor(out=norms[:], in0=held["norm_sq", g][:], in1=half[:], op=ALU.pow)
            held["norms", g] = norms

        def clip_denominator(g):
            denom = small.tile([P, GROUP], F32)
            em, hm = held["norms", g][:, 0, :], held["norms", g][:, 1, :]
            for j in range(GROUP):
                nc.vector.tensor_scalar(
                    out=denom[:, j : j + 1], in0=hm[:, j : j + 1], scalar1=BAG_EPS, scalar2=em[:, j : j + 1],
                    op0=ALU.add, op1=ALU.max,
                )
            held["denom", g] = denom

        def clip_reciprocal(g):
            recip = small.tile([P, GROUP], F32)
            nc.vector.reciprocal(out=recip[:], in_=held["denom", g][:])
            held["recip", g] = recip

        def clip_factor(g):
            alpha = small.tile([P, GROUP], F32)
            em = held["norms", g][:, 0, :]
            for j in range(GROUP):
                nc.vector.tensor_scalar_mul(
                    out=alpha[:, j : j + 1], in0=held["recip", g][:, j : j + 1], scalar1=em[:, j : j + 1]
                )
            held["alpha", g] = alpha

        def clip(g, j):
            pre = work.tile([P, H], F32, bufs=4)
            pre_sum = small.tile([P, 1], F32)
            nc.vector.scalar_tensor_tensor(
                out=pre[:], in0=held["h", g, j][:], scalar=held["alpha", g][:, j : j + 1], in1=rows_of("main", g, j),
                op0=ALU.mult, op1=ALU.add, accum_out=pre_sum[:],
            )
            held["pre", g, j], held["pre_sum", g, j] = pre, pre_sum

        def mean(g, j):
            negmu = small.tile([P, 1], F32)
            nc.vector.tensor_scalar_mul(out=negmu[:], in0=held["pre_sum", g, j][:], scalar1=-1.0 / H)
            held["negmu", g, j] = negmu

        def centre(g, j):
            centred = work.tile([P, H], F32, bufs=3)
            nc.vector.scalar_tensor_tensor(
                out=centred[:], in0=held["pre", g, j][:], scalar=held["negmu", g, j][:], in1=gain[:], op0=ALU.add, op1=ALU.mult
            )
            held["centred", g, j] = centred

        def deviation(g, j):
            if j == 0:
                dev_sq = small.tile([P, GROUP], F32)
                held["dev_sq", g] = dev_sq
            unread_p = work.tile([P, H], BF16, tag="unread", bufs=4)
            nc.scalar.activation(
                out=unread_p[:], in_=held["pre", g, j][:], func=ACT.Square, bias=held["negmu", g, j][:],
                accum_out=held["dev_sq", g][:, j : j + 1],
            )

        def variance(g):
            var_eps = small.tile([P, GROUP], F32)
            nc.gpsimd.tensor_scalar(
                out=var_eps[:], in0=held["dev_sq", g][:], scalar1=1.0 / H, scalar2=LN_EPS, op0=ALU.mult, op1=ALU.add
            )
            held["var_eps", g] = var_eps

        def inv_std(g):
            rstd = small.tile([P, GROUP], F32)
            nc.gpsimd.tensor_tensor(out=rstd[:], in0=held["var_eps", g][:], in1=minus_half[:], op=ALU.pow)
            factor = small.tile([P, GROUP], F32)
            nc.gpsimd.tensor_mul(out=factor[:], in0=rstd[:], in1=bag[:, g * GROUP : (g + 1) * GROUP])
            held["factor", g] = factor

        def blend(g, j):
            t = g * GROUP + j
            shift_c = work.tile([P, H], F32, bufs=5)
            nc.vector.scalar_tensor_tensor(
                out=shift_c[:], in0=held["centred", g, j][:], scalar=held["factor", g][:, j : j + 1], in1=held["wm", g, j][:],
                op0=ALU.mult, op1=ALU.add,
            )
            nc.sync.dma_start(out=shift_v[:, t, :], in_=shift_c[:])
            held["shift_c", g, j] = shift_c

        def squash(g, j):
            tanh_c = work.tile([P, H], F32, bufs=3)
            nc.scalar.activation(out=tanh_c[:], in_=held["shift_c", g, j][:], func=ACT.Tanh)
            held["tanh_c", g, j] = tanh_c

        def gate_out(g, j):
            h_sb = work.tile([P, H], F32, bufs=3)
            engine = nc.gpsimd if g * GROUP + j < TILES - LAST else nc.vector
            engine.tensor_tensor(out=h_sb[:], in0=held["tanh_c", g, j][:], in1=rows_of("o", g, j), op=ALU.mult)
            nc.sync.dma_start(out=h_v[:, g * GROUP + j, :], in_=h_sb[:])

        def per_tile(step, lag, *stages):
            t = step - lag
            if 0 <= t < TILES:
                for stage in stages:
                    stage(t // GROUP, t % GROUP)

        def per_group(step, lag, *stages):
            t = step - lag
            if 0 <= t < TILES and t % GROUP == 0:
                for stage in stages:
                    stage(t // GROUP)

        for step in range(TILES + AT_OUT):
            for b in range(len(LOADS) - 1):
                if max(LOADS[b] - LOAD_AHEAD, 0) == step:
                    load(b)
                    if b == 1:
                        load_words()
                    if b == 2:
                        load_scales()
            for b in range(TILES // LOAD):
                if b * LOAD - LOAD_O_AHEAD + AT_OUT == step:
                    load_o(b)
            per_group(step, AT_ALPHA, roots)
            per_tile(step, AT_PRODUCT, product(0))
            per_tile(step, AT_TURN, transpose_in)
            if step == GROUP:
                prepare_biases()
            if step == 2 * GROUP:
                prepare_bag()
            if step == AT_CLIP:
                prepare_gain()
            per_tile(step, AT_NORM_H, transpose_back)
            per_tile(step, AT_NORM_MAIN, norm_main)
            per_tile(step, AT_KEPT, kept)
            per_group(step, AT_ALPHA, clip_denominator)
            per_tile(step, AT_DEVIATION, mean)
            per_tile(step, AT_PRODUCT, product(1))
            per_group(step, AT_VARIANCE, variance, inv_std)
            per_tile(step, AT_TURN, copy_in)
            per_tile(step, AT_NORM_H, norm_h)
            per_tile(step, AT_DEVIATION, deviation)
            per_group(step, AT_ALPHA, clip_reciprocal)
            per_tile(step, AT_MATMUL, gate_matmuls, relu_gate)
            per_tile(step, AT_CENTRE, centre)
            per_group(step, AT_ALPHA, clip_factor)
            per_tile(step, AT_KEPT - 1, bag_shift)
            per_tile(step, AT_SQUASH, squash)
            per_tile(step, AT_OUT, gate_out)
            per_group(step, AT_QUANTISE, quantise)
            per_tile(step, AT_CLIP, clip)
            per_tile(step, AT_BLEND, blend)
